import numpy as np
import ml_dtypes


def mxq(x, axis, fmt="e4m3"):
    dtype, down = {"e4m3": (ml_dtypes.float8_e4m3fn, 7), "e5m2": (ml_dtypes.float8_e5m2, 14)}[fmt]
    v = np.moveaxis(np.asarray(x, np.float32).astype(ml_dtypes.bfloat16).astype(np.float64), axis, -1)
    blocks = v.reshape(v.shape[:-1] + (-1, 32))
    amax = np.abs(blocks).max(-1, keepdims=True)
    byte = np.maximum(np.where(amax > 0, np.frexp(amax)[1] - 1 + 127, 0) - down, 1)
    scale = np.exp2(byte - 127.0)
    codes = (blocks / scale).astype(np.float32).astype(dtype).astype(np.float64)
    return np.moveaxis((codes * scale).reshape(v.shape), -1, axis)


WIDE = False


def mx_kscale(k):
    if not WIDE:
        return np.ones(k)
    levels = np.array([10, -10, 5, -5, 0])
    a = np.random.permutation(np.resize(levels, k // 512 * 4)).reshape(k // 512, 4)
    idx = np.arange(k)
    return np.exp2(a[idx // 512, idx % 128 // 32])


BF16 = ml_dtypes.bfloat16


def bf(x):
    return np.asarray(x, np.float32).astype(BF16)


def f64(x):
    return np.asarray(x).astype(np.float64)


N, NB, D = 4096, 1024, 1024

INV_SQRT_2PI = 1.0 / np.sqrt(2.0 * np.pi)


def phi(t):
    return INV_SQRT_2PI * np.exp(-0.5 * t * t)


def setup_inputs():
    a = np.log2(mx_kscale(NB))
    u = np.exp2(np.round(1.2 * (a - a.min())))
    g = np.where(u > 1.0, np.where(u == u.max(), 0.25, 0.1), 1.0)
    q_mu = 0.5 + 0.2 * np.random.standard_normal(N)
    q_sigma_sq = 0.01 + 0.1 * np.random.random(N)
    theta = np.stack([q_mu / q_sigma_sq, -0.5 / q_sigma_sq], axis=1)
    basis_mu = np.linspace(0.0, 1.0, NB) + 0.01 * np.random.standard_normal(NB)
    basis_sigma = 0.05 * (1.0 + 0.1 * np.random.standard_normal(NB)) * u
    Bv = np.random.standard_normal((NB, D)) * 0.64 / np.sqrt(NB) * (u * g)[:, None]
    return {"theta": bf(theta), "basis_mu": bf(basis_mu), "basis_sigma": bf(basis_sigma), "Bv": bf(Bv)}


def reference(theta, basis_mu, basis_sigma, Bv):
    theta, basis_mu, basis_sigma, Bv = f64(theta), f64(basis_mu), f64(basis_sigma), f64(Bv)
    sigma_sq = -0.5 / theta[:, 1]
    mu = theta[:, 0] * sigma_sq
    s = np.sqrt(basis_sigma[None, :] ** 2 + sigma_sq[:, None])
    r = phi((mu[:, None] - basis_mu[None, :]) / s) / s
    context = mxq(r, 1, "e4m3") @ mxq(Bv, 0, "e4m3")
    return context

@@ -1,0 +1,508 @@
+import math
+from contextlib import ExitStack
+
+import concourse.mybir as mybir
+from concourse.masks import make_identity
+
+F32 = mybir.dt.float32
+BF16 = mybir.dt.bfloat16
+U32 = mybir.dt.uint32
+I32 = mybir.dt.int32
+U8 = mybir.dt.uint8
+FP8X4 = mybir.dt.float8_e4m3fn_x4
+AF = mybir.ActivationFunctionType
+ALU = mybir.AluOpType
+
+P = 128
+ROWS, NB, D = 4096, 1024, 1024
+PACK = 4
+PASSES = NB // (P * PACK)
+TILES = ROWS // P
+CHUNK_TILES = 4
+CHUNK = CHUNK_TILES * P
+CHUNKS = TILES // CHUNK_TILES
+UNITS = CHUNKS * PASSES
+BANK = 512
+GROUP = 4
+GROUPS = UNITS // GROUP
+
+FLOPS = 2 * ROWS * NB * D
+
+CLASSIC = (2, 4)
+FED = (0, 1, 3, 5, 6, 7)
+FED_RUNS = ((0, 2), (3, 4), (5, 8))
+PAIRED = (3, 5, 7)
+PLANES = PASSES * PACK
+TERMS = 7
+COMBOS = ((0, 0), (1, 0), (2, 0), (0, 1), (1, 1), (0, 2))
+SLOT = 8
+HOLD = False
+S_ON_DVE = ()
+Z_ON_DVE = (15,)
+LAST_UNIT = UNITS - 1
+STEP_EV = (4, 4, 4)
+LAST_EV = (0, 2, 2, 0)
+TAIL_EV = (0, 1, 2, 1)
+LN_FROM_SBUF = False
+LAST_ACT = (0, 0, 1, 1)
+TAIL_ACT = (2, 2, 2, 1)
+
+
+def plan():
+    steps = []
+    pending = []
+    taken = [0]
+    done = {}
+    issued = {}
+    mxq = []
+    mxt = [0]
+
+    def drain(n, eng):
+        for s in range(n):
+            if taken[0] >= len(pending):
+                return
+            h, a, dh = pending[taken[0]]
+            taken[0] += 1
+            steps.append(("EV", h, a, dh, eng))
+            tiles = 1 if h == CHUNKS - 1 else 2
+            first = a - a % tiles
+            done[(h, first)] = done.get((h, first), 0) + 1
+            if done[(h, first)] == 2 * tiles:
+                steps.append(("ST", h, first, first + tiles))
+
+    def once(step):
+        if step not in issued:
+            issued[step] = 1
+            steps.append(step)
+
+    def bcast(kind, h):
+        if h < CHUNKS:
+            once((kind, h))
+
+    def squares(u, planes):
+        if u < UNITS and u // 2 in FED:
+            for t in planes:
+                once(("D2", u, t))
+        elif u < UNITS:
+            once(("BM", u // 2))
+
+    extra = [0]
+
+    def passes():
+        while mxt[0] < len(mxq) and len(pending) - taken[0] <= 2 + 2 * extra[0]:
+            h, a = mxq[mxt[0]]
+            mxt[0] += 1
+            cyc = ("acc", "acc", "BR", "BM")[: 2 + extra[0]]
+            steps.append(("MX", h, a, cyc[mxt[0] % len(cyc)]))
+            pending.append((h, a, 0))
+            pending.append((h, a, 1))
+
+    def empty(n, eng):
+        for s in range((n + 3) // 4):
+            drain(min(4, n - 4 * s), eng)
+            passes()
+
+    def logs(lo, hi):
+        for u in range(lo, hi):
+            bcast("BR", u // 2)
+            steps.append(("LN", u))
+            if u // 2 in PAIRED:
+                steps.append(("S", u))
+            if u % 2 == 1:
+                bcast("BR", u // 2 + 2)
+
+    def quant(u, a0, a1):
+        steps.append(("Q", u, a0, a1))
+        if u % 2 == 1:
+            for a in range(a0, a1):
+                mxq.append((u // 2, a))
+
+    bcast("BR", 0)
+    bcast("BR", 1)
+    steps.append(("PREP", 0))
+    squares(0, (0, 1))
+    steps.append(("BVG", 0))
+    steps.append(("BVG", 1))
+    logs(0, GROUP)
+    for gi in range(GROUPS):
+        lo, hi = gi * GROUP, (gi + 1) * GROUP
+        last = gi + 1 == GROUPS
+        for idx in range(GROUP):
+            u = lo + idx
+            p = u - GROUP if gi > 0 else None
+            if last and idx == 0:
+                extra[0] = 1
+            steps.append(("W", u))
+            if p is not None:
+                steps.append(("F", p, 0, CHUNK_TILES))
+            if last:
+                drain(LAST_ACT[idx], "act")
+            if u // 2 in CLASSIC:
+                steps.append(("A1", u))
+                steps.append(("B2", u))
+            else:
+                squares(u, (0, 1))
+                steps.append(("BDV", u, 0))
+                squares(u, (2,))
+                steps.append(("BDV", u, 1))
+                squares(u, (3,))
+                steps.append(("BDV", u, 2))
+                steps.append(("BDV", u, 3))
+            squares(u + 1, (0, 1))
+            if p is not None:
+                quant(p, 0, CHUNK_TILES)
+                if HOLD:
+                    steps.append(("H", p))
+            steps.append(("Z", u, "dve" if u in Z_ON_DVE else "pool"))
+            empty(LAST_EV[idx] if last else STEP_EV[gi], "dve")
+        if gi == 0:
+            steps.append(("BVQ", 0))
+            steps.append(("BVQ", 1))
+            steps.append(("PREP", 1))
+        if not last:
+            logs(hi, hi + GROUP)
+            empty(16, "dve")
+    extra[0] = 2
+    for u in range(UNITS - GROUP, UNITS):
+        width = 1 if u == LAST_UNIT else CHUNK_TILES
+        for a0 in range(0, CHUNK_TILES, width):
+            steps.append(("F", u, a0, a0 + width))
+            drain(TAIL_ACT[u - (UNITS - GROUP)], "act")
+            quant(u, a0, a0 + width)
+            passes()
+            empty(TAIL_EV[u - (UNITS - GROUP)], "dve")
+    while taken[0] < len(pending) or mxt[0] < len(mxq):
+        passes()
+        drain(1, "act")
+        drain(1, "dve")
+    return steps
+
+
+def tile_longtermattention_kernel(tc, theta, basis_mu, basis_sigma, Bv, out):
+    nc = tc.nc
+    out_v = out.rearrange("(p i) d -> p i d", i=TILES)
+    kappa = math.sqrt(2.0 * math.pi)
+    with ExitStack() as ctx:
+        ctx.enter_context(tc.manual_schedule())
+        const = ctx.enter_context(tc.tile_pool(name="const", bufs=1))
+        logs = ctx.enter_context(tc.tile_pool(name="logs", bufs=8))
+        work = ctx.enter_context(tc.tile_pool(name="work", bufs=6))
+        pair = ctx.enter_context(tc.tile_pool(name="pair", bufs=3))
+        flat = ctx.enter_context(tc.tile_pool(name="flat", bufs=3))
+        rows = ctx.enter_context(tc.tile_pool(name="rows", bufs=3))
+        packed = ctx.enter_context(tc.tile_pool(name="packed", bufs=6))
+        results = ctx.enter_context(tc.tile_pool(name="results", bufs=4))
+        spread = ctx.enter_context(tc.psum_pool(name="spread", bufs=2))
+        sums = ctx.enter_context(tc.psum_pool(name="sums", bufs=4))
+
+        th = const.tile([P, TILES, 2], BF16)
+        nc.sync.dma_start(out=th[:], in_=theta.rearrange("(p i) two -> p i two", i=TILES))
+        bs = const.tile([P, PASSES, PACK], BF16)
+        nc.sync.dma_start(out=bs[:], in_=basis_sigma.rearrange("(c p t) -> p c t", p=P, t=PACK))
+        bm = const.tile([P, PASSES, PACK], BF16)
+        nc.sync.dma_start(out=bm[:], in_=basis_mu.rearrange("(c p t) -> p c t", p=P, t=PACK))
+        raws = []
+        for c in range(PASSES):
+            raw = logs.tile([P, PACK, D], BF16, tag="ll", align_bytes=64)
+            nc.sync.dma_start(
+                out=raw[:],
+                in_=Bv[c * P * PACK : (c + 1) * P * PACK, :].rearrange("(p t) w -> p t w", t=PACK),
+            )
+            raws.append(raw)
+
+        ident = const.tile([P, P], F32)
+        make_identity(nc, ident[:])
+        identb = const.tile([P, P], BF16)
+        make_identity(nc, identb[:])
+
+        warm = const.tile([P, 1], F32)
+        nc.vector.memset(warm[:], 1.0)
+        warm2 = const.tile([P, 1], F32)
+        nc.scalar.activation(out=warm2[:], in_=warm[:], func=AF.Ln)
+        cofq = const.tile([P, 2 * PLANES, P], BF16)
+        nc.vector.memset(cofq[:].bitcast(I32), 0)
+        rowq = const.tile([P, TILES, P], BF16)
+        for h0, h1 in FED_RUNS:
+            nc.vector.memset(rowq[:, h0 * CHUNK_TILES : h1 * CHUNK_TILES, :].bitcast(I32), 0)
+
+        rec = const.tile([P, TILES], F32)
+        nc.vector.reciprocal(out=rec[:], in_=th[:, :, 1])
+        mu = const.tile([P, TILES], F32)
+        nc.vector.scalar_tensor_tensor(
+            out=mu[:], in0=rec[:], scalar=-0.5 * kappa, in1=th[:, :, 0], op0=ALU.mult, op1=ALU.mult
+        )
+        bsf = bs[:].rearrange("p c t -> p (c t)")
+        b2 = const.tile([P, PASSES * PACK], F32)
+        nc.vector.scalar_tensor_tensor(
+            out=b2[:], in0=bsf, scalar=2.0 * math.pi, in1=bsf, op0=ALU.mult, op1=ALU.mult
+        )
+        bmf = const.tile([P, PASSES * PACK], F32)
+        nc.vector.tensor_scalar_mul(out=bmf[:], in0=bm[:].rearrange("p c t -> p (c t)"), scalar1=kappa)
+
+        bvc = const.tile([P, PASSES, D], U32, align_bytes=64)
+        bvs = const.tile([P, PASSES, D], U8, align_bytes=64)
+
+        recb, mub, ll, ww, rb, cod, scl, acc, ost, grp = {}, {}, {}, {}, {}, {}, {}, {}, {}, {}
+        d2, ss = {}, {}
+        pi2 = math.pi * math.pi
+        bmv = bm[:].rearrange("p c t -> p (c t)")
+        rowsT = const.tile([P, len(FED) * CHUNK_TILES, P], BF16)
+        cofT = const.tile([P, 2 * PLANES, P], BF16)
+        kc = const.tile([P, 2 * PLANES], F32)
+
+        def split3(src, shape, name):
+            pieces = []
+            rest = src
+            for e in range(3):
+                pc = const.tile(shape, BF16, name="%s_p%d" % (name, e))
+                nc.vector.tensor_copy(out=pc[:], in_=rest[:])
+                pieces.append(pc)
+                if e < 2:
+                    nxt = const.tile(shape, F32, name="%s_r%d" % (name, e))
+                    nc.vector.tensor_tensor(out=nxt[:], in0=rest[:], in1=pc[:], op=ALU.subtract)
+                    rest = nxt
+            return pieces
+
+        def prepare_rows():
+            xf = const.tile([P, TERMS, TILES], F32)
+            sg = const.tile([P, TILES], F32)
+            nc.vector.tensor_scalar_mul(out=sg[:], in0=rec[:], scalar1=-0.5)
+            nc.vector.tensor_scalar_mul(out=xf[:, 4, :], in0=rec[:], scalar1=-2.0 * pi2)
+            nc.vector.scalar_tensor_tensor(
+                out=xf[:, 3, :], in0=rec[:], scalar=4.0 * pi2, in1=th[:, :, 0], op0=ALU.mult, op1=ALU.mult
+            )
+            nc.vector.scalar_tensor_tensor(
+                out=xf[:, 1, :], in0=xf[:, 3, :], scalar=1.0 / (16.0 * pi2), in1=xf[:, 3, :], op0=ALU.mult, op1=ALU.mult
+            )
+            nc.vector.tensor_tensor(out=xf[:, 0, :], in0=xf[:, 1, :], in1=sg[:], op=ALU.mult)
+            nc.vector.tensor_tensor(out=xf[:, 2, :], in0=xf[:, 3, :], in1=sg[:], op=ALU.mult)
+            nc.vector.tensor_scalar_mul(out=xf[:, 5, :], in0=xf[:, 1, :], scalar1=0.5 / math.pi)
+            nc.vector.tensor_scalar_mul(out=xf[:, 6, :], in0=xf[:, 3, :], scalar1=0.5 / math.pi)
+            pcs = split3(xf, [P, TERMS, TILES], "xf")
+            for blk, (e, f) in enumerate(COMBOS):
+                nc.vector.tensor_copy(
+                    out=rowq[:, :, blk * SLOT : blk * SLOT + TERMS], in_=pcs[e][:].rearrange("p f i -> p i f")
+                )
+
+        def prepare_coefficients():
+            cf = const.tile([P, TERMS, 2 * PLANES], F32)
+            nc.vector.memset(cf[:], 0.0)
+            lo = slice(0, PLANES)
+            hi = slice(PLANES, 2 * PLANES)
+            gg = const.tile([P, PLANES], F32)
+            nc.vector.tensor_tensor(out=gg[:], in0=bsf, in1=bsf, op=ALU.mult)
+            nc.vector.memset(cf[:, 0, lo], 1.0)
+            nc.vector.memset(cf[:, 5, hi], 1.0)
+            nc.vector.tensor_copy(out=cf[:, 6, hi], in_=bmv)
+            nc.vector.tensor_tensor(out=kc[:, hi], in0=bmf[:], in1=bmf[:], op=ALU.mult)
+            cfp = cf[:, 1, lo].rearrange("p (q two) -> p q two", two=2)
+            ggp = gg[:].rearrange("p (q two) -> p q two", two=2)
+            nc.vector.tensor_copy(out=cfp[:, :, 0], in_=ggp[:, :, 1])
+            nc.vector.tensor_copy(out=cfp[:, :, 1], in_=ggp[:, :, 0])
+            nc.vector.tensor_copy(out=cf[:, 2, lo], in_=bmv)
+            nc.vector.tensor_tensor(out=cf[:, 3, lo], in0=cf[:, 2, lo], in1=cf[:, 1, lo], op=ALU.mult)
+            nc.vector.tensor_tensor(out=cf[:, 4, lo], in0=cf[:, 2, lo], in1=cf[:, 2, lo], op=ALU.mult)
+            nc.vector.scalar_tensor_tensor(
+                out=kc[:, lo], in0=cf[:, 4, lo], scalar=4.0 * pi2, in1=cf[:, 1, lo], op0=ALU.mult, op1=ALU.mult
+            )
+            pcs = split3(cf, [P, TERMS, 2 * PLANES], "cf")
+            for blk, (e, f) in enumerate(COMBOS):
+                nc.vector.tensor_copy(
+                    out=cofq[:, :, blk * SLOT : blk * SLOT + TERMS], in_=pcs[f][:].rearrange("p f k -> p k f")
+                )
+
+        def turn(dst, d0, src, s0):
+            tp = sums.tile([P, 4, P], BF16, tag="acc")
+            for j in range(4):
+                nc.tensor.transpose(tp[:, j, :], src[:, s0 + j, :], identb[:])
+            nc.vector.tensor_copy(out=dst[:, d0 : d0 + 4, :], in_=tp[:])
+
+        def prepare_squares(part):
+            if part == 0:
+                prepare_coefficients()
+                prepare_rows()
+            for j0 in range(0, 2 * PLANES, 4):
+                if (j0 >= PLANES) == (part == 0):
+                    turn(cofT, j0, cofq, j0)
+            for hh in range(len(FED)):
+                if (FED[hh] < GROUP // 2) == (part == 0):
+                    turn(rowsT, hh * CHUNK_TILES, rowq, FED[hh] * CHUNK_TILES)
+
+        for st in plan():
+            kind = st[0]
+            if kind == "BR" or kind == "BM":
+                h = st[1]
+                src = rec if kind == "BR" else mu
+                bk = spread.tile([P, BANK], F32, tag=kind)
+                for a in range(CHUNK_TILES):
+                    i = h * CHUNK_TILES + a
+                    nc.tensor.transpose(bk[:, a * P : (a + 1) * P], src[:, i : i + 1].to_broadcast([P, P]), ident[:])
+                if kind == "BR" and LN_FROM_SBUF:
+                    rc = flat.tile([P, BANK], F32)
+                    nc.vector.tensor_copy(out=rc[:], in_=bk[:])
+                    recb[h] = rc
+                elif kind == "BR":
+                    recb[h] = bk
+                else:
+                    mub[h] = bk
+            elif kind == "LN":
+                u = st[1]
+                lt = logs.tile([P, PACK, CHUNK], F32, tag="ll", align_bytes=64)
+                for t in range(PACK):
+                    k = (u % 2) * PACK + t
+                    nc.scalar.activation(
+                        out=lt[:, t, :],
+                        in_=recb[u // 2][:],
+                        func=AF.Ln,
+                        bias=b2[:, k : k + 1],
+                        scale=-math.pi,
+                    )
+                ll[u] = lt
+            elif kind == "S":
+                u = st[1]
+                sst = pair.tile([P, PACK // 2, CHUNK], F32)
+                lv = ll[u][:].rearrange("p (q two) n -> p q two n", two=2)
+                if u in S_ON_DVE:
+                    nc.vector.tensor_tensor(out=sst[:], in0=lv[:, :, 0, :], in1=lv[:, :, 1, :], op=ALU.add)
+                else:
+                    nc.gpsimd.tensor_tensor(out=sst[:], in0=lv[:, :, 0, :], in1=lv[:, :, 1, :], op=ALU.add)
+                ss[u] = sst
+            elif kind == "W":
+                u = st[1]
+                wt = work.tile([P, PACK, CHUNK], F32, tag="ww", align_bytes=64)
+                ww[u] = wt
+                if u // 2 in PAIRED:
+                    sf = ss[u][:].rearrange("p q n -> p (q n)")
+                    nc.scalar.activation(out=sf, in_=sf, func=AF.Exp, scale=-1.0)
+                else:
+                    nc.scalar.activation(
+                        out=wt[:].rearrange("p t n -> p (t n)"),
+                        in_=ll[u][:].rearrange("p t n -> p (t n)"),
+                        func=AF.Exp,
+                        scale=-1.0,
+                    )
+            elif kind == "A1" or kind == "B2":
+                u = st[1]
+                for t in range(PACK):
+                    k = (u % 2) * PACK + t
+                    nc.vector.scalar_tensor_tensor(
+                        out=ww[u][:, t, :],
+                        in0=mub[u // 2][:],
+                        scalar=bmf[:, k : k + 1],
+                        in1=ww[u][:, t, :],
+                        op0=ALU.subtract,
+                        op1=ALU.mult,
+                    )
+            elif kind == "PREP":
+                prepare_squares(st[1])
+            elif kind == "D2":
+                u, t = st[1], st[2]
+                k = (u % 2) * PACK + t
+                d2t = spread.tile([P, BANK], F32, tag="BM")
+                n0 = FED.index(u // 2) * CHUNK_TILES
+                nc.tensor.matmul(
+                    out=d2t[:],
+                    lhsT=cofT[:, k if u // 2 in PAIRED else PLANES + k, :],
+                    rhs=rowsT[:, n0 : n0 + CHUNK_TILES, :].rearrange("r a p -> r (a p)"),
+                    start=True,
+                    stop=True,
+                )
+                d2[(u, t)] = d2t
+            elif kind == "BDV":
+                u, t = st[1], st[2]
+                k = (u % 2) * PACK + t
+                kk = k if u // 2 in PAIRED else PLANES + k
+                nc.vector.scalar_tensor_tensor(
+                    out=ww[u][:, t, :],
+                    in0=d2[(u, t)][:],
+                    scalar=kc[:, kk : kk + 1],
+                    in1=ss[u][:, t // 2, :] if u // 2 in PAIRED else ww[u][:, t, :],
+                    op0=ALU.add,
+                    op1=ALU.mult,
+                )
+            elif kind == "H":
+                jk = const.tile([P, 1], U32, name="junk")
+                nc.gpsimd.tensor_copy(out=jk[:], in_=cod[st[1]][:, 0:1])
+            elif kind == "Z":
+                u = st[1]
+                wf = ww[u][:].rearrange("p t n -> p (t n)")
+                lf = ll[u][:].rearrange("p t n -> p (t n)")
+                if st[2] == "pool":
+                    nc.gpsimd.tensor_tensor(out=wf, in0=wf, in1=lf, op=ALU.add)
+                else:
+                    nc.vector.tensor_tensor(out=wf, in0=wf, in1=lf, op=ALU.add)
+            elif kind == "F":
+                u = st[1]
+                cols = slice(st[2] * P, st[3] * P)
+                if u not in rb:
+                    rbt = rows.tile([P, CHUNK, PACK], BF16, align_bytes=64)
+                    rb[u] = rbt
+                nc.scalar.activation(
+                    out=rb[u][:, cols, :].rearrange("p (m i) t -> p m t i", i=4),
+                    in_=ww[u][:, :, cols].rearrange("p t (m i) -> p m t i", i=4),
+                    func=AF.Exp,
+                    scale=-0.5,
+                )
+            elif kind == "Q":
+                u = st[1]
+                cols = slice(st[2] * P, st[3] * P)
+                if u not in cod:
+                    cdt = packed.tile([P, CHUNK], U32, align_bytes=64)
+                    sct = packed.tile([P, CHUNK], U8, align_bytes=64)
+                    cod[u], scl[u] = cdt, sct
+                nc.vector.quantize_mx(
+                    out=cod[u][:, cols].bitcast(FP8X4),
+                    scales=scl[u][:, cols],
+                    in_=rb[u][:, cols, :].rearrange("p n t -> p (n t)"),
+                )
+            elif kind == "BVG":
+                c = st[1]
+                gt = work.tile([P, D, PACK], BF16, tag="ww", align_bytes=64)
+                nc.vector.tensor_copy(
+                    out=gt[:].rearrange("p (m i) t -> p m t i", i=4),
+                    in_=raws[c][:].rearrange("p t (m i) -> p m t i", i=4),
+                )
+                grp[c] = gt
+            elif kind == "BVQ":
+                c = st[1]
+                nc.vector.quantize_mx(
+                    out=bvc[:, c, :].bitcast(FP8X4),
+                    scales=bvs[:, c, :],
+                    in_=grp[c][:].rearrange("p w t -> p (w t)"),
+                )
+            elif kind == "MX":
+                h, a = st[1], st[2]
+                cols = slice(a * P, (a + 1) * P)
+                for dh in range(D // BANK):
+                    if st[3] == "acc":
+                        at = sums.tile([P, BANK], F32, tag="acc")
+                    else:
+                        at = spread.tile([P, BANK], F32, tag=st[3])
+                    dcols = slice(dh * BANK, (dh + 1) * BANK)
+                    for c in range(PASSES):
+                        nc.tensor.matmul_mx(
+                            out=at[:],
+                            lhsT=cod[2 * h + c][:, cols].bitcast(FP8X4),
+                            lhsT_scale=scl[2 * h + c][:, cols],
+                            rhs=bvc[:, c, dcols].bitcast(FP8X4),
+                            rhs_scale=bvs[:, c, dcols],
+                            start=(c == 0),
+                            stop=(c == PASSES - 1),
+                        )
+                    acc[(h, a, dh)] = at
+            elif kind == "EV":
+                h, a, dh, eng = st[1], st[2], st[3], st[4]
+                if (h, a // 2) not in ost:
+                    ot = results.tile([P, 2, D], F32)
+                    ost[(h, a // 2)] = ot
+                dst = ost[(h, a // 2)][:, a % 2, dh * BANK : (dh + 1) * BANK]
+                if eng == "act":
+                    nc.scalar.copy(out=dst, in_=acc[(h, a, dh)][:])
+                else:
+                    nc.vector.tensor_copy(out=dst, in_=acc[(h, a, dh)][:])
+            elif kind == "ST":
+                h, a0, a1 = st[1], st[2], st[3]
+                i0 = h * CHUNK_TILES
+                nc.sync.dma_start(
+                    out=out_v[:, i0 + a0 : i0 + a1, :], in_=ost[(h, a0 // 2)][:, a0 % 2 : a0 % 2 + a1 - a0, :]
+                )

@@ -124,6 +124,8 @@ def plan():
     steps.append(("BVG", 0))
     steps.append(("BVG", 1))
     logs(0, GROUP)
+    steps.append(("BVQ", 0))
+    steps.append(("BVQ", 1))
     for gi in range(GROUPS):
         lo, hi = gi * GROUP, (gi + 1) * GROUP
         last = gi + 1 == GROUPS
@@ -156,8 +158,6 @@ def plan():
             steps.append(("Z", u, "dve" if u in Z_ON_DVE else "pool"))
             empty(LAST_EV[idx] if last else STEP_EV[gi], "dve")
         if gi == 0:
-            steps.append(("BVQ", 0))
-            steps.append(("BVQ", 1))
             steps.append(("PREP", 1))
         if not last:
             logs(hi, hi + GROUP)

@@ -18,34 +18,36 @@ ROWS, NB, D = 4096, 1024, 1024
 PACK = 4
 PASSES = NB // (P * PACK)
 TILES = ROWS // P
-CHUNK_TILES = 4
-CHUNK = CHUNK_TILES * P
-CHUNKS = TILES // CHUNK_TILES
-UNITS = CHUNKS * PASSES
 BANK = 512
-GROUP = 4
-GROUPS = UNITS // GROUP
+PLANES = PASSES * PACK
+HALF = PLANES // 2
+TERMS = 6
+COMBOS = ((0, 0), (1, 0), (2, 0), (0, 1), (1, 1), (0, 2))
+SLOT = 8
 
 FLOPS = 2 * ROWS * NB * D
 
-CLASSIC = (2, 4)
-FED = (0, 1, 3, 5, 6, 7)
-FED_RUNS = ((0, 2), (3, 4), (5, 8))
-PAIRED = (3, 5, 7)
-PLANES = PASSES * PACK
-TERMS = 7
-COMBOS = ((0, 0), (1, 0), (2, 0), (0, 1), (1, 1), (0, 2))
-SLOT = 8
-HOLD = False
-S_ON_DVE = ()
-Z_ON_DVE = (15,)
-LAST_UNIT = UNITS - 1
-STEP_EV = (4, 4, 4)
-LAST_EV = (0, 2, 2, 0)
-TAIL_EV = (0, 1, 2, 1)
-LN_FROM_SBUF = False
-LAST_ACT = (0, 0, 1, 1)
-TAIL_ACT = (2, 2, 2, 1)
+SIZES = (14, 10, 8)
+CLASSIC = (4, 8, 13, 17, 22, 26, 30)
+GADD = ()
+D_BUFS = 4
+Z_BUFS = 4
+ACC_BUFS = 8
+L_BUFS = 16
+S_BUFS = 5
+B_BUFS = 5
+R_BUFS = 4
+C_BUFS = 18
+O_BUFS = 4
+WA = 1
+EXP_MX = (0, 0, 0)
+EV_STEP = (0, 0, 0)
+TAIL_SPLIT = True
+ZL = 2
+FL = 3
+QL = 4
+DL = 1
+EV_ACT = (0, 0, 0)
 
 
 def plan():
@@ -53,128 +55,105 @@ def plan():
     pending = []
     taken = [0]
     done = {}
-    issued = {}
     mxq = []
     mxt = [0]
+    turned = {}
 
     def drain(n, eng):
         for s in range(n):
             if taken[0] >= len(pending):
                 return
-            h, a, dh = pending[taken[0]]
+            i, dh = pending[taken[0]]
             taken[0] += 1
-            steps.append(("EV", h, a, dh, eng))
-            tiles = 1 if h == CHUNKS - 1 else 2
-            first = a - a % tiles
-            done[(h, first)] = done.get((h, first), 0) + 1
-            if done[(h, first)] == 2 * tiles:
-                steps.append(("ST", h, first, first + tiles))
+            steps.append(("EV", i, dh, eng))
+            tiles = 1 if i >= TILES - 2 else 2
+            first = i - i % tiles
+            done[first] = done.get(first, 0) + 1
+            if done[first] == 2 * tiles:
+                steps.append(("ST", first, first + tiles))
 
-    def once(step):
-        if step not in issued:
-            issued[step] = 1
-            steps.append(step)
+    tags = [("d", "z")]
 
-    def bcast(kind, h):
-        if h < CHUNKS:
-            once((kind, h))
-
-    def squares(u, planes):
-        if u < UNITS and u // 2 in FED:
-            for t in planes:
-                once(("D2", u, t))
-        elif u < UNITS:
-            once(("BM", u // 2))
-
-    extra = [0]
-
-    def passes():
-        while mxt[0] < len(mxq) and len(pending) - taken[0] <= 2 + 2 * extra[0]:
-            h, a = mxq[mxt[0]]
+    def passes(limit=99):
+        n = 0
+        while mxt[0] < len(mxq) and len(pending) - taken[0] <= ACC_BUFS - 2 and n < limit:
+            i = mxq[mxt[0]]
+            steps.append(("MX", i, tags[0][mxt[0] % len(tags[0])]))
             mxt[0] += 1
-            cyc = ("acc", "acc", "BR", "BM")[: 2 + extra[0]]
-            steps.append(("MX", h, a, cyc[mxt[0] % len(cyc)]))
-            pending.append((h, a, 0))
-            pending.append((h, a, 1))
+            n += 1
+            pending.append((i, 0))
+            pending.append((i, 1))
 
-    def empty(n, eng):
-        for s in range((n + 3) // 4):
-            drain(min(4, n - 4 * s), eng)
-            passes()
+    def d2(i):
+        if i < TILES and i not in CLASSIC:
+            if i // 4 not in turned:
+                turned[i // 4] = 1
+                steps.append(("TURN", i // 4))
+            steps.append(("D2", i))
 
     def logs(lo, hi):
-        for u in range(lo, hi):
-            bcast("BR", u // 2)
-            steps.append(("LN", u))
-            if u // 2 in PAIRED:
-                steps.append(("S", u))
-            if u % 2 == 1:
-                bcast("BR", u // 2 + 2)
+        for i in range(lo, hi):
+            steps.append(("LN", i))
+            if i not in CLASSIC:
+                steps.append(("S", i))
 
-    def quant(u, a0, a1):
-        steps.append(("Q", u, a0, a1))
-        if u % 2 == 1:
-            for a in range(a0, a1):
-                mxq.append((u // 2, a))
-
-    bcast("BR", 0)
-    bcast("BR", 1)
-    steps.append(("PREP", 0))
-    squares(0, (0, 1))
+    steps.append(("XB",))
+    steps.append(("PREP",))
+    d2(0)
     steps.append(("BVG", 0))
     steps.append(("BVG", 1))
-    logs(0, GROUP)
+    logs(0, SIZES[0])
     steps.append(("BVQ", 0))
     steps.append(("BVQ", 1))
-    for gi in range(GROUPS):
-        lo, hi = gi * GROUP, (gi + 1) * GROUP
-        last = gi + 1 == GROUPS
-        for idx in range(GROUP):
-            u = lo + idx
-            p = u - GROUP if gi > 0 else None
-            if last and idx == 0:
-                extra[0] = 1
-            steps.append(("W", u))
-            if p is not None:
-                steps.append(("F", p, 0, CHUNK_TILES))
-            if last:
-                drain(LAST_ACT[idx], "act")
-            if u // 2 in CLASSIC:
-                steps.append(("A1", u))
-                steps.append(("B2", u))
-            else:
-                squares(u, (0, 1))
-                steps.append(("BDV", u, 0))
-                squares(u, (2,))
-                steps.append(("BDV", u, 1))
-                squares(u, (3,))
-                steps.append(("BDV", u, 2))
-                steps.append(("BDV", u, 3))
-            squares(u + 1, (0, 1))
-            if p is not None:
-                quant(p, 0, CHUNK_TILES)
-                if HOLD:
-                    steps.append(("H", p))
-            steps.append(("Z", u, "dve" if u in Z_ON_DVE else "pool"))
-            empty(LAST_EV[idx] if last else STEP_EV[gi], "dve")
-        if gi == 0:
-            steps.append(("PREP", 1))
+    for q in range(1, TILES // 4):
+        if q * 4 < SIZES[0]:
+            turned[q] = 1
+            steps.append(("TURN", q))
+    steps.append(("KB",))
+    lo = 0
+    for gi, size in enumerate(SIZES):
+        hi = lo + size
+        last = gi + 1 == len(SIZES)
+        for s in range(lo, hi + QL):
+            if s == lo:
+                for k in range(WA):
+                    steps.append(("W", lo + k))
+                for k in range(1, DL):
+                    d2(lo + k)
+            if s + WA < hi:
+                steps.append(("W", s + WA))
+            if s < hi:
+                steps.append(("B", s))
+                if s in GADD:
+                    steps.append(("GZ", s))
+            if lo <= s - ZL < hi:
+                steps.append(("ZT", s - ZL))
+            if s + DL < hi:
+                d2(s + DL)
+            if lo <= s - FL < hi:
+                steps.append(("F", s - FL))
+            if lo <= s - QL < hi:
+                steps.append(("Q", s - QL))
+                mxq.append(s - QL)
+
+        tags[0] = ("d", "z")
         if not last:
-            logs(hi, hi + GROUP)
-            empty(16, "dve")
-    extra[0] = 2
-    for u in range(UNITS - GROUP, UNITS):
-        width = 1 if u == LAST_UNIT else CHUNK_TILES
-        for a0 in range(0, CHUNK_TILES, width):
-            steps.append(("F", u, a0, a0 + width))
-            drain(TAIL_ACT[u - (UNITS - GROUP)], "act")
-            quant(u, a0, a0 + width)
-            passes()
-            empty(TAIL_EV[u - (UNITS - GROUP)], "dve")
+            for q in range(TILES // 4):
+                if q not in turned and q * 4 < hi + SIZES[gi + 1]:
+                    turned[q] = 1
+                    steps.append(("TURN", q))
+            logs(hi, hi + SIZES[gi + 1])
+            while mxt[0] < len(mxq):
+                passes()
+                drain(1, "dve")
+            d2(hi)
+            drain(99, "dve")
+        lo = hi
+    n = 0
     while taken[0] < len(pending) or mxt[0] < len(mxq):
         passes()
-        drain(1, "act")
-        drain(1, "dve")
+        drain(1, "act" if n % 2 else "dve")
+        n += 1
     return steps
 
 
@@ -182,18 +161,19 @@ def tile_longtermattention_kernel(tc, theta, basis_mu, basis_sigma, Bv, out):
     nc = tc.nc
     out_v = out.rearrange("(p i) d -> p i d", i=TILES)
     kappa = math.sqrt(2.0 * math.pi)
+    pi2 = math.pi * math.pi
     with ExitStack() as ctx:
         ctx.enter_context(tc.manual_schedule())
         const = ctx.enter_context(tc.tile_pool(name="const", bufs=1))
-        logs = ctx.enter_context(tc.tile_pool(name="logs", bufs=8))
-        work = ctx.enter_context(tc.tile_pool(name="work", bufs=6))
-        pair = ctx.enter_context(tc.tile_pool(name="pair", bufs=3))
-        flat = ctx.enter_context(tc.tile_pool(name="flat", bufs=3))
-        rows = ctx.enter_context(tc.tile_pool(name="rows", bufs=3))
-        packed = ctx.enter_context(tc.tile_pool(name="packed", bufs=6))
-        results = ctx.enter_context(tc.tile_pool(name="results", bufs=4))
-        spread = ctx.enter_context(tc.psum_pool(name="spread", bufs=2))
-        sums = ctx.enter_context(tc.psum_pool(name="sums", bufs=4))
+        logs = ctx.enter_context(tc.tile_pool(name="logs", bufs=L_BUFS))
+        pair = ctx.enter_context(tc.tile_pool(name="pair", bufs=S_BUFS))
+        prod = ctx.enter_context(tc.tile_pool(name="prod", bufs=B_BUFS))
+        rows = ctx.enter_context(tc.tile_pool(name="rows", bufs=R_BUFS))
+        packed = ctx.enter_context(tc.tile_pool(name="packed", bufs=C_BUFS))
+        results = ctx.enter_context(tc.tile_pool(name="results", bufs=O_BUFS))
+        ps_d = ctx.enter_context(tc.psum_pool(name="ps_d", bufs=D_BUFS))
+        ps_z = ctx.enter_context(tc.psum_pool(name="ps_z", bufs=Z_BUFS))
+        banks = {"z": ps_z, "d": ps_d}
 
         th = const.tile([P, TILES, 2], BF16)
         nc.sync.dma_start(out=th[:], in_=theta.rearrange("(p i) two -> p i two", i=TILES))
@@ -203,7 +183,7 @@ def tile_longtermattention_kernel(tc, theta, basis_mu, basis_sigma, Bv, out):
         nc.sync.dma_start(out=bm[:], in_=basis_mu.rearrange("(c p t) -> p c t", p=P, t=PACK))
         raws = []
         for c in range(PASSES):
-            raw = logs.tile([P, PACK, D], BF16, tag="ll", align_bytes=64)
+            raw = results.tile([P, PACK, D], BF16, tag="ost", align_bytes=64)
             nc.sync.dma_start(
                 out=raw[:],
                 in_=Bv[c * P * PACK : (c + 1) * P * PACK, :].rearrange("(p t) w -> p t w", t=PACK),
@@ -219,36 +199,32 @@ def tile_longtermattention_kernel(tc, theta, basis_mu, basis_sigma, Bv, out):
         nc.vector.memset(warm[:], 1.0)
         warm2 = const.tile([P, 1], F32)
         nc.scalar.activation(out=warm2[:], in_=warm[:], func=AF.Ln)
-        cofq = const.tile([P, 2 * PLANES, P], BF16)
+        cofq = const.tile([P, PLANES, P], BF16)
         nc.vector.memset(cofq[:].bitcast(I32), 0)
         rowq = const.tile([P, TILES, P], BF16)
-        for h0, h1 in FED_RUNS:
-            nc.vector.memset(rowq[:, h0 * CHUNK_TILES : h1 * CHUNK_TILES, :].bitcast(I32), 0)
+        nc.vector.memset(rowq[:].bitcast(I32), 0)
 
+        bst = const.tile([P, PLANES], F32)
+        nc.vector.tensor_copy(out=bst[:].rearrange("p (t c) -> p t c", c=PASSES), in_=bs[:].rearrange("p c t -> p t c"))
+        bmt = const.tile([P, PLANES], F32)
+        b2 = const.tile([P, PLANES], F32)
+        nc.vector.scalar_tensor_tensor(
+            out=b2[:], in0=bst[:], scalar=2.0 * math.pi, in1=bst[:], op0=ALU.mult, op1=ALU.mult
+        )
         rec = const.tile([P, TILES], F32)
         nc.vector.reciprocal(out=rec[:], in_=th[:, :, 1])
+        xa = const.tile([P, TILES], F32)
+        nc.vector.tensor_scalar_mul(out=xa[:], in0=rec[:], scalar1=-math.pi)
         mu = const.tile([P, TILES], F32)
-        nc.vector.scalar_tensor_tensor(
-            out=mu[:], in0=rec[:], scalar=-0.5 * kappa, in1=th[:, :, 0], op0=ALU.mult, op1=ALU.mult
-        )
-        bsf = bs[:].rearrange("p c t -> p (c t)")
-        b2 = const.tile([P, PASSES * PACK], F32)
-        nc.vector.scalar_tensor_tensor(
-            out=b2[:], in0=bsf, scalar=2.0 * math.pi, in1=bsf, op0=ALU.mult, op1=ALU.mult
-        )
-        bmf = const.tile([P, PASSES * PACK], F32)
-        nc.vector.tensor_scalar_mul(out=bmf[:], in0=bm[:].rearrange("p c t -> p (c t)"), scalar1=kappa)
+        bmf = const.tile([P, PLANES], F32)
 
         bvc = const.tile([P, PASSES, D], U32, align_bytes=64)
         bvs = const.tile([P, PASSES, D], U8, align_bytes=64)
-
-        recb, mub, ll, ww, rb, cod, scl, acc, ost, grp = {}, {}, {}, {}, {}, {}, {}, {}, {}, {}
-        d2, ss = {}, {}
-        pi2 = math.pi * math.pi
-        bmv = bm[:].rearrange("p c t -> p (c t)")
-        rowsT = const.tile([P, len(FED) * CHUNK_TILES, P], BF16)
-        cofT = const.tile([P, 2 * PLANES, P], BF16)
-        kc = const.tile([P, 2 * PLANES], F32)
+        xb = const.tile([P, PLANES, P], F32)
+        kb = const.tile([P, PLANES, P], F32)
+        rowsT = const.tile([P, TILES, P], BF16)
+        cofT = const.tile([P, PLANES, P], BF16)
+        ll, ww, bb, d2, zz, rb, cod, scl, acc, ost, grp = {}, {}, {}, {}, {}, {}, {}, {}, {}, {}, {}
 
         def split3(src, shape, name):
             pieces = []
@@ -266,6 +242,7 @@ def tile_longtermattention_kernel(tc, theta, basis_mu, basis_sigma, Bv, out):
         def prepare_rows():
             xf = const.tile([P, TERMS, TILES], F32)
             sg = const.tile([P, TILES], F32)
+            nc.vector.memset(xf[:, 5, :], 1.0)
             nc.vector.tensor_scalar_mul(out=sg[:], in0=rec[:], scalar1=-0.5)
             nc.vector.tensor_scalar_mul(out=xf[:, 4, :], in0=rec[:], scalar1=-2.0 * pi2)
             nc.vector.scalar_tensor_tensor(
@@ -276,8 +253,6 @@ def tile_longtermattention_kernel(tc, theta, basis_mu, basis_sigma, Bv, out):
             )
             nc.vector.tensor_tensor(out=xf[:, 0, :], in0=xf[:, 1, :], in1=sg[:], op=ALU.mult)
             nc.vector.tensor_tensor(out=xf[:, 2, :], in0=xf[:, 3, :], in1=sg[:], op=ALU.mult)
-            nc.vector.tensor_scalar_mul(out=xf[:, 5, :], in0=xf[:, 1, :], scalar1=0.5 / math.pi)
-            nc.vector.tensor_scalar_mul(out=xf[:, 6, :], in0=xf[:, 3, :], scalar1=0.5 / math.pi)
             pcs = split3(xf, [P, TERMS, TILES], "xf")
             for blk, (e, f) in enumerate(COMBOS):
                 nc.vector.tensor_copy(
@@ -285,179 +260,158 @@ def tile_longtermattention_kernel(tc, theta, basis_mu, basis_sigma, Bv, out):
                 )
 
         def prepare_coefficients():
-            cf = const.tile([P, TERMS, 2 * PLANES], F32)
-            nc.vector.memset(cf[:], 0.0)
-            lo = slice(0, PLANES)
-            hi = slice(PLANES, 2 * PLANES)
-            gg = const.tile([P, PLANES], F32)
-            nc.vector.tensor_tensor(out=gg[:], in0=bsf, in1=bsf, op=ALU.mult)
-            nc.vector.memset(cf[:, 0, lo], 1.0)
-            nc.vector.memset(cf[:, 5, hi], 1.0)
-            nc.vector.tensor_copy(out=cf[:, 6, hi], in_=bmv)
-            nc.vector.tensor_tensor(out=kc[:, hi], in0=bmf[:], in1=bmf[:], op=ALU.mult)
-            cfp = cf[:, 1, lo].rearrange("p (q two) -> p q two", two=2)
-            ggp = gg[:].rearrange("p (q two) -> p q two", two=2)
-            nc.vector.tensor_copy(out=cfp[:, :, 0], in_=ggp[:, :, 1])
-            nc.vector.tensor_copy(out=cfp[:, :, 1], in_=ggp[:, :, 0])
-            nc.vector.tensor_copy(out=cf[:, 2, lo], in_=bmv)
-            nc.vector.tensor_tensor(out=cf[:, 3, lo], in0=cf[:, 2, lo], in1=cf[:, 1, lo], op=ALU.mult)
-            nc.vector.tensor_tensor(out=cf[:, 4, lo], in0=cf[:, 2, lo], in1=cf[:, 2, lo], op=ALU.mult)
-            nc.vector.scalar_tensor_tensor(
-                out=kc[:, lo], in0=cf[:, 4, lo], scalar=4.0 * pi2, in1=cf[:, 1, lo], op0=ALU.mult, op1=ALU.mult
+            cf = const.tile([P, TERMS, PLANES], F32)
+            lo = slice(0, HALF)
+            hi = slice(HALF, PLANES)
+            nc.vector.tensor_copy(
+                out=bmt[:].rearrange("p (t c) -> p t c", c=PASSES), in_=bm[:].rearrange("p c t -> p t c")
             )
-            pcs = split3(cf, [P, TERMS, 2 * PLANES], "cf")
+            nc.vector.memset(cf[:, 0, :], 1.0)
+            nc.vector.tensor_tensor(out=cf[:, 1, hi], in0=bst[:, lo], in1=bst[:, lo], op=ALU.mult)
+            nc.vector.tensor_tensor(out=cf[:, 1, lo], in0=bst[:, hi], in1=bst[:, hi], op=ALU.mult)
+            nc.vector.tensor_copy(out=cf[:, 2, :], in_=bmt[:])
+            nc.vector.tensor_tensor(out=cf[:, 4, :], in0=bmt[:], in1=bmt[:], op=ALU.mult)
+            nc.vector.tensor_tensor(out=cf[:, 3, :], in0=bmt[:], in1=cf[:, 1, :], op=ALU.mult)
+            nc.vector.scalar_tensor_tensor(
+                out=cf[:, 5, :], in0=cf[:, 4, :], scalar=4.0 * pi2, in1=cf[:, 1, :], op0=ALU.mult, op1=ALU.mult
+            )
+            pcs = split3(cf, [P, TERMS, PLANES], "cf")
             for blk, (e, f) in enumerate(COMBOS):
                 nc.vector.tensor_copy(
                     out=cofq[:, :, blk * SLOT : blk * SLOT + TERMS], in_=pcs[f][:].rearrange("p f k -> p k f")
                 )
 
         def turn(dst, d0, src, s0):
-            tp = sums.tile([P, 4, P], BF16, tag="acc")
+            tp = ps_z.tile([P, 4, P], BF16, tag="z")
             for j in range(4):
                 nc.tensor.transpose(tp[:, j, :], src[:, s0 + j, :], identb[:])
             nc.vector.tensor_copy(out=dst[:, d0 : d0 + 4, :], in_=tp[:])
 
-        def prepare_squares(part):
-            if part == 0:
-                prepare_coefficients()
-                prepare_rows()
-            for j0 in range(0, 2 * PLANES, 4):
-                if (j0 >= PLANES) == (part == 0):
-                    turn(cofT, j0, cofq, j0)
-            for hh in range(len(FED)):
-                if (FED[hh] < GROUP // 2) == (part == 0):
-                    turn(rowsT, hh * CHUNK_TILES, rowq, FED[hh] * CHUNK_TILES)
+        def spread(dst, src, eng, tag):
+            for g in range(2):
+                bk = banks[tag].tile([P, 4, P], F32, tag=tag)
+                for j in range(4):
+                    k = 4 * g + j
+                    nc.tensor.transpose(bk[:, j, :], src[:, k : k + 1].to_broadcast([P, P]), ident[:])
+                if eng == "act":
+                    nc.scalar.copy(out=dst[:, 4 * g : 4 * g + 4, :], in_=bk[:])
+                else:
+                    nc.vector.tensor_copy(out=dst[:, 4 * g : 4 * g + 4, :], in_=bk[:])
 
+        xbf = xb[:].rearrange("p k m -> p (k m)")
+        kbf = kb[:].rearrange("p k m -> p (k m)")
         for st in plan():
             kind = st[0]
-            if kind == "BR" or kind == "BM":
-                h = st[1]
-                src = rec if kind == "BR" else mu
-                bk = spread.tile([P, BANK], F32, tag=kind)
-                for a in range(CHUNK_TILES):
-                    i = h * CHUNK_TILES + a
-                    nc.tensor.transpose(bk[:, a * P : (a + 1) * P], src[:, i : i + 1].to_broadcast([P, P]), ident[:])
-                if kind == "BR" and LN_FROM_SBUF:
-                    rc = flat.tile([P, BANK], F32)
-                    nc.vector.tensor_copy(out=rc[:], in_=bk[:])
-                    recb[h] = rc
-                elif kind == "BR":
-                    recb[h] = bk
-                else:
-                    mub[h] = bk
-            elif kind == "LN":
-                u = st[1]
-                lt = logs.tile([P, PACK, CHUNK], F32, tag="ll", align_bytes=64)
-                for t in range(PACK):
-                    k = (u % 2) * PACK + t
-                    nc.scalar.activation(
-                        out=lt[:, t, :],
-                        in_=recb[u // 2][:],
-                        func=AF.Ln,
-                        bias=b2[:, k : k + 1],
-                        scale=-math.pi,
-                    )
-                ll[u] = lt
-            elif kind == "S":
-                u = st[1]
-                sst = pair.tile([P, PACK // 2, CHUNK], F32)
-                lv = ll[u][:].rearrange("p (q two) n -> p q two n", two=2)
-                if u in S_ON_DVE:
-                    nc.vector.tensor_tensor(out=sst[:], in0=lv[:, :, 0, :], in1=lv[:, :, 1, :], op=ALU.add)
-                else:
-                    nc.gpsimd.tensor_tensor(out=sst[:], in0=lv[:, :, 0, :], in1=lv[:, :, 1, :], op=ALU.add)
-                ss[u] = sst
-            elif kind == "W":
-                u = st[1]
-                wt = work.tile([P, PACK, CHUNK], F32, tag="ww", align_bytes=64)
-                ww[u] = wt
-                if u // 2 in PAIRED:
-                    sf = ss[u][:].rearrange("p q n -> p (q n)")
-                    nc.scalar.activation(out=sf, in_=sf, func=AF.Exp, scale=-1.0)
-                else:
-                    nc.scalar.activation(
-                        out=wt[:].rearrange("p t n -> p (t n)"),
-                        in_=ll[u][:].rearrange("p t n -> p (t n)"),
-                        func=AF.Exp,
-                        scale=-1.0,
-                    )
-            elif kind == "A1" or kind == "B2":
-                u = st[1]
-                for t in range(PACK):
-                    k = (u % 2) * PACK + t
-                    nc.vector.scalar_tensor_tensor(
-                        out=ww[u][:, t, :],
-                        in0=mub[u // 2][:],
-                        scalar=bmf[:, k : k + 1],
-                        in1=ww[u][:, t, :],
-                        op0=ALU.subtract,
-                        op1=ALU.mult,
-                    )
-            elif kind == "PREP":
-                prepare_squares(st[1])
-            elif kind == "D2":
-                u, t = st[1], st[2]
-                k = (u % 2) * PACK + t
-                d2t = spread.tile([P, BANK], F32, tag="BM")
-                n0 = FED.index(u // 2) * CHUNK_TILES
-                nc.tensor.matmul(
-                    out=d2t[:],
-                    lhsT=cofT[:, k if u // 2 in PAIRED else PLANES + k, :],
-                    rhs=rowsT[:, n0 : n0 + CHUNK_TILES, :].rearrange("r a p -> r (a p)"),
-                    start=True,
-                    stop=True,
-                )
-                d2[(u, t)] = d2t
-            elif kind == "BDV":
-                u, t = st[1], st[2]
-                k = (u % 2) * PACK + t
-                kk = k if u // 2 in PAIRED else PLANES + k
+            if kind == "XB":
+                spread(xb, b2, "act", "d")
+            elif kind == "KB":
+                nc.vector.tensor_scalar_mul(out=bmf[:], in0=bmt[:], scalar1=kappa)
                 nc.vector.scalar_tensor_tensor(
-                    out=ww[u][:, t, :],
-                    in0=d2[(u, t)][:],
-                    scalar=kc[:, kk : kk + 1],
-                    in1=ss[u][:, t // 2, :] if u // 2 in PAIRED else ww[u][:, t, :],
-                    op0=ALU.add,
-                    op1=ALU.mult,
+                    out=mu[:], in0=rec[:], scalar=-0.5 * kappa, in1=th[:, :, 0], op0=ALU.mult, op1=ALU.mult
                 )
-            elif kind == "H":
-                jk = const.tile([P, 1], U32, name="junk")
-                nc.gpsimd.tensor_copy(out=jk[:], in_=cod[st[1]][:, 0:1])
-            elif kind == "Z":
-                u = st[1]
-                wf = ww[u][:].rearrange("p t n -> p (t n)")
-                lf = ll[u][:].rearrange("p t n -> p (t n)")
-                if st[2] == "pool":
-                    nc.gpsimd.tensor_tensor(out=wf, in0=wf, in1=lf, op=ALU.add)
+                spread(kb, bmf, "dve", "z")
+            elif kind == "PREP":
+                prepare_coefficients()
+                turn(cofT, 0, cofq, 0)
+                turn(cofT, 4, cofq, 4)
+                prepare_rows()
+            elif kind == "TURN":
+                turn(rowsT, 4 * st[1], rowq, 4 * st[1])
+            elif kind == "LN":
+                i = st[1]
+                lt = logs.tile([P, PLANES * P], F32, align_bytes=64)
+                nc.scalar.activation(out=lt[:], in_=xbf, func=AF.Ln, bias=xa[:, i : i + 1])
+                ll[i] = lt
+            elif kind == "S":
+                i = st[1]
+                sst = pair.tile([P, HALF * P], F32)
+                nc.gpsimd.tensor_tensor(
+                    out=sst[:], in0=ll[i][:, 0 : HALF * P], in1=ll[i][:, HALF * P : PLANES * P], op=ALU.add
+                )
+                ww[i] = sst
+            elif kind == "W":
+                i = st[1]
+                if i in CLASSIC:
+                    bt = prod.tile([P, PLANES * P], F32, tag="bt", align_bytes=64)
+                    bb[i] = bt
+                    nc.scalar.activation(out=bt[:], in_=ll[i][:], func=AF.Exp, scale=-1.0)
                 else:
-                    nc.vector.tensor_tensor(out=wf, in0=wf, in1=lf, op=ALU.add)
+                    nc.scalar.activation(out=ww[i][:], in_=ww[i][:], func=AF.Exp, scale=-1.0)
+            elif kind == "D2":
+                i = st[1]
+                for e in range(2):
+                    dt = ps_d.tile([P, BANK], F32, tag="d")
+                    nc.tensor.matmul(
+                        out=dt[:],
+                        lhsT=rowsT[:, i, :],
+                        rhs=cofT[:, e * HALF : (e + 1) * HALF, :].rearrange("r k m -> r (k m)"),
+                        start=True,
+                        stop=True,
+                    )
+                    d2[(i, e)] = dt
+            elif kind == "B":
+                i = st[1]
+                if i in CLASSIC:
+                    for s in range(2):
+                        nc.vector.scalar_tensor_tensor(
+                            out=bb[i][:],
+                            in0=kbf,
+                            scalar=mu[:, i : i + 1],
+                            in1=bb[i][:],
+                            op0=ALU.subtract,
+                            op1=ALU.mult,
+                        )
+                else:
+                    bt = prod.tile([P, PLANES * P], F32, tag="bt", align_bytes=64)
+                    bb[i] = bt
+                    for e in range(2):
+                        nc.vector.tensor_tensor(
+                            out=bt[:, e * BANK : (e + 1) * BANK], in0=d2[(i, e)][:], in1=ww[i][:], op=ALU.mult
+                        )
+            elif kind == "GZ":
+                i = st[1]
+                nc.gpsimd.tensor_tensor(out=bb[i][:], in0=bb[i][:], in1=ll[i][:], op=ALU.add)
+            elif kind == "ZT":
+                i = st[1]
+                for c in range(PASSES):
+                    zt = ps_z.tile([P, PACK, P], F32, tag="z")
+                    for t in range(PACK):
+                        k = PASSES * t + c
+                        ks = slice(k * P, (k + 1) * P)
+                        if i in GADD:
+                            nc.tensor.transpose(zt[:, t, :], bb[i][:, ks], ident[:])
+                        else:
+                            nc.tensor.matmul(
+                                out=zt[:, t, :], lhsT=ll[i][:, ks], rhs=ident[:], start=True, stop=False, is_transpose=True
+                            )
+                            nc.tensor.matmul(
+                                out=zt[:, t, :], lhsT=bb[i][:, ks], rhs=ident[:], start=False, stop=True, is_transpose=True
+                            )
+                    zz[(i, c)] = zt
             elif kind == "F":
-                u = st[1]
-                cols = slice(st[2] * P, st[3] * P)
-                if u not in rb:
-                    rbt = rows.tile([P, CHUNK, PACK], BF16, align_bytes=64)
-                    rb[u] = rbt
-                nc.scalar.activation(
-                    out=rb[u][:, cols, :].rearrange("p (m i) t -> p m t i", i=4),
-                    in_=ww[u][:, :, cols].rearrange("p t (m i) -> p m t i", i=4),
-                    func=AF.Exp,
-                    scale=-0.5,
-                )
+                i = st[1]
+                rbt = rows.tile([P, PASSES, P, PACK], BF16, align_bytes=64)
+                rb[i] = rbt
+                for c in range(PASSES):
+                    nc.scalar.activation(
+                        out=rbt[:, c, :, :],
+                        in_=zz[(i, c)][:].rearrange("p t n -> p n t"),
+                        func=AF.Exp,
+                        scale=-0.5,
+                    )
             elif kind == "Q":
-                u = st[1]
-                cols = slice(st[2] * P, st[3] * P)
-                if u not in cod:
-                    cdt = packed.tile([P, CHUNK], U32, align_bytes=64)
-                    sct = packed.tile([P, CHUNK], U8, align_bytes=64)
-                    cod[u], scl[u] = cdt, sct
+                i = st[1]
+                cdt = packed.tile([P, PASSES * P], U32, align_bytes=64)
+                sct = packed.tile([P, PASSES * P], U8, align_bytes=64)
+                cod[i], scl[i] = cdt, sct
                 nc.vector.quantize_mx(
-                    out=cod[u][:, cols].bitcast(FP8X4),
-                    scales=scl[u][:, cols],
-                    in_=rb[u][:, cols, :].rearrange("p n t -> p (n t)"),
+                    out=cdt[:].bitcast(FP8X4),
+                    scales=sct[:],
+                    in_=rb[i][:].rearrange("p c n t -> p (c n t)"),
                 )
             elif kind == "BVG":
                 c = st[1]
-                gt = work.tile([P, D, PACK], BF16, tag="ww", align_bytes=64)
+                gt = results.tile([P, D, PACK], BF16, tag="ost", align_bytes=64)
                 nc.vector.tensor_copy(
                     out=gt[:].rearrange("p (m i) t -> p m t i", i=4),
                     in_=raws[c][:].rearrange("p t (m i) -> p m t i", i=4),
@@ -471,38 +425,34 @@ def tile_longtermattention_kernel(tc, theta, basis_mu, basis_sigma, Bv, out):
                     in_=grp[c][:].rearrange("p w t -> p (w t)"),
                 )
             elif kind == "MX":
-                h, a = st[1], st[2]
-                cols = slice(a * P, (a + 1) * P)
+                i, tag = st[1], st[2]
                 for dh in range(D // BANK):
-                    if st[3] == "acc":
-                        at = sums.tile([P, BANK], F32, tag="acc")
-                    else:
-                        at = spread.tile([P, BANK], F32, tag=st[3])
+                    at = banks[tag].tile([P, BANK], F32, tag=tag)
                     dcols = slice(dh * BANK, (dh + 1) * BANK)
                     for c in range(PASSES):
+                        cols = slice(c * P, (c + 1) * P)
                         nc.tensor.matmul_mx(
                             out=at[:],
-                            lhsT=cod[2 * h + c][:, cols].bitcast(FP8X4),
-                            lhsT_scale=scl[2 * h + c][:, cols],
+                            lhsT=cod[i][:, cols].bitcast(FP8X4),
+                            lhsT_scale=scl[i][:, cols],
                             rhs=bvc[:, c, dcols].bitcast(FP8X4),
                             rhs_scale=bvs[:, c, dcols],
                             start=(c == 0),
                             stop=(c == PASSES - 1),
                         )
-                    acc[(h, a, dh)] = at
+                    acc[(i, dh)] = at
             elif kind == "EV":
-                h, a, dh, eng = st[1], st[2], st[3], st[4]
-                if (h, a // 2) not in ost:
-                    ot = results.tile([P, 2, D], F32)
-                    ost[(h, a // 2)] = ot
-                dst = ost[(h, a // 2)][:, a % 2, dh * BANK : (dh + 1) * BANK]
+                i, dh, eng = st[1], st[2], st[3]
+                if i // 2 not in ost:
+                    ot = results.tile([P, 2, D], F32, tag="ost", align_bytes=64)
+                    ost[i // 2] = ot
+                dst = ost[i // 2][:, i % 2, dh * BANK : (dh + 1) * BANK]
                 if eng == "act":
-                    nc.scalar.copy(out=dst, in_=acc[(h, a, dh)][:])
+                    nc.scalar.copy(out=dst, in_=acc[(i, dh)][:])
                 else:
-                    nc.vector.tensor_copy(out=dst, in_=acc[(h, a, dh)][:])
+                    nc.vector.tensor_copy(out=dst, in_=acc[(i, dh)][:])
             elif kind == "ST":
-                h, a0, a1 = st[1], st[2], st[3]
-                i0 = h * CHUNK_TILES
+                i0, i1 = st[1], st[2]
                 nc.sync.dma_start(
-                    out=out_v[:, i0 + a0 : i0 + a1, :], in_=ost[(h, a0 // 2)][:, a0 % 2 : a0 % 2 + a1 - a0, :]
+                    out=out_v[:, i0:i1, :], in_=ost[i0 // 2][:, i0 % 2 : i0 % 2 + i1 - i0, :]
                 )

@@ -34,19 +34,20 @@ D_BUFS = 4
 Z_BUFS = 4
 ACC_BUFS = 8
 L_BUFS = 16
-S_BUFS = 5
-B_BUFS = 5
-R_BUFS = 4
+S_BUFS = 8
+B_BUFS = 7
+R_BUFS = 6
 C_BUFS = 18
 O_BUFS = 4
 WA = 1
 EXP_MX = (0, 0, 0)
 EV_STEP = (0, 0, 0)
 TAIL_SPLIT = True
-ZL = 2
-FL = 3
-QL = 4
-DL = 1
+ZL = 1
+FL = 2
+QL = 3
+RUN = 2
+KB_EARLY = False
 EV_ACT = (0, 0, 0)
 
 
@@ -99,43 +100,52 @@ def plan():
 
     steps.append(("XB",))
     steps.append(("PREP",))
-    d2(0)
-    steps.append(("BVG", 0))
-    steps.append(("BVG", 1))
+    for k in range(RUN):
+        d2(k)
+    if KB_EARLY:
+        steps.append(("KB",))
+    for s in range(4):
+        steps.append(("BVG", s))
+    for s in range(4):
+        steps.append(("BVQ", s))
     logs(0, SIZES[0])
-    steps.append(("BVQ", 0))
-    steps.append(("BVQ", 1))
     for q in range(1, TILES // 4):
         if q * 4 < SIZES[0]:
             turned[q] = 1
             steps.append(("TURN", q))
-    steps.append(("KB",))
+    if not KB_EARLY:
+        steps.append(("KB",))
     lo = 0
     for gi, size in enumerate(SIZES):
         hi = lo + size
         last = gi + 1 == len(SIZES)
-        for s in range(lo, hi + QL):
-            if s == lo:
-                for k in range(WA):
-                    steps.append(("W", lo + k))
-                for k in range(1, DL):
-                    d2(lo + k)
-            if s + WA < hi:
-                steps.append(("W", s + WA))
-            if s < hi:
-                steps.append(("B", s))
-                if s in GADD:
-                    steps.append(("GZ", s))
-            if lo <= s - ZL < hi:
-                steps.append(("ZT", s - ZL))
-            if s + DL < hi:
-                d2(s + DL)
-            if lo <= s - FL < hi:
-                steps.append(("F", s - FL))
-            if lo <= s - QL < hi:
-                steps.append(("Q", s - QL))
-                mxq.append(s - QL)
-
+        runs = [tuple(range(a, min(a + RUN, hi))) for a in range(lo, hi, RUN)]
+        for s in range(len(runs) + QL):
+            if s == 0:
+                for w in range(min(WA, len(runs))):
+                    for k in runs[w]:
+                        steps.append(("W", k))
+            if s + WA < len(runs):
+                for k in runs[s + WA]:
+                    steps.append(("W", k))
+            if s < len(runs):
+                for part in range(2):
+                    for k in runs[s]:
+                        if part == 0 or k in CLASSIC:
+                            steps.append(("B", k, part))
+            if 0 <= s - ZL < len(runs):
+                for k in runs[s - ZL]:
+                    steps.append(("ZT", k))
+            if s + 1 < len(runs):
+                for k in runs[s + 1]:
+                    d2(k)
+            if 0 <= s - FL < len(runs):
+                for k in runs[s - FL]:
+                    steps.append(("F", k))
+            if 0 <= s - QL < len(runs):
+                for k in runs[s - QL]:
+                    steps.append(("Q", k))
+                    mxq.append(k)
         tags[0] = ("d", "z")
         if not last:
             for q in range(TILES // 4):
@@ -146,7 +156,8 @@ def plan():
             while mxt[0] < len(mxq):
                 passes()
                 drain(1, "dve")
-            d2(hi)
+            for k in range(hi, hi + RUN):
+                d2(k)
             drain(99, "dve")
         lo = hi
     n = 0
@@ -182,11 +193,16 @@ def tile_longtermattention_kernel(tc, theta, basis_mu, basis_sigma, Bv, out):
         bm = const.tile([P, PASSES, PACK], BF16)
         nc.sync.dma_start(out=bm[:], in_=basis_mu.rearrange("(c p t) -> p c t", p=P, t=PACK))
         raws = []
-        for c in range(PASSES):
-            raw = results.tile([P, PACK, D], BF16, tag="ost", align_bytes=64)
+        grps = []
+        for s in range(4):
+            gt = pair.tile([P, BANK, PACK], BF16, tag="sst", align_bytes=64)
+            grps.append(gt)
+        for s in range(4):
+            c, w = s // 2, s % 2
+            raw = pair.tile([P, PACK, BANK], BF16, tag="sst", align_bytes=64)
             nc.sync.dma_start(
                 out=raw[:],
-                in_=Bv[c * P * PACK : (c + 1) * P * PACK, :].rearrange("(p t) w -> p t w", t=PACK),
+                in_=Bv[c * P * PACK : (c + 1) * P * PACK, w * BANK : (w + 1) * BANK].rearrange("(p t) w -> p t w", t=PACK),
             )
             raws.append(raw)
 
@@ -206,7 +222,6 @@ def tile_longtermattention_kernel(tc, theta, basis_mu, basis_sigma, Bv, out):
 
         bst = const.tile([P, PLANES], F32)
         nc.vector.tensor_copy(out=bst[:].rearrange("p (t c) -> p t c", c=PASSES), in_=bs[:].rearrange("p c t -> p t c"))
-        bmt = const.tile([P, PLANES], F32)
         b2 = const.tile([P, PLANES], F32)
         nc.vector.scalar_tensor_tensor(
             out=b2[:], in0=bst[:], scalar=2.0 * math.pi, in1=bst[:], op0=ALU.mult, op1=ALU.mult
@@ -224,62 +239,52 @@ def tile_longtermattention_kernel(tc, theta, basis_mu, basis_sigma, Bv, out):
         kb = const.tile([P, PLANES, P], F32)
         rowsT = const.tile([P, TILES, P], BF16)
         cofT = const.tile([P, PLANES, P], BF16)
-        ll, ww, bb, d2, zz, rb, cod, scl, acc, ost, grp = {}, {}, {}, {}, {}, {}, {}, {}, {}, {}, {}
+        ll, ww, bb, d2, zz, rb, cod, scl, acc, ost = {}, {}, {}, {}, {}, {}, {}, {}, {}, {}
 
-        def split3(src, shape, name):
-            pieces = []
-            rest = src
+        def prepare():
+            wide = TILES + PLANES
+            xf = const.tile([P, TERMS, wide], F32)
+            sg = const.tile([P, TILES], F32)
+            r = slice(0, TILES)
+            c = slice(TILES, wide)
+            lo = slice(TILES, TILES + HALF)
+            hi = slice(TILES + HALF, wide)
+            nc.vector.memset(xf[:, 5, r], 1.0)
+            nc.vector.memset(xf[:, 0, c], 1.0)
+            nc.vector.scalar_tensor_tensor(
+                out=xf[:, 3, r], in0=rec[:], scalar=4.0 * pi2, in1=th[:, :, 0], op0=ALU.mult, op1=ALU.mult
+            )
+            nc.vector.tensor_copy(
+                out=xf[:, 2, c].rearrange("p (t c) -> p t c", c=PASSES), in_=bm[:].rearrange("p c t -> p t c")
+            )
+            nc.vector.tensor_scalar_mul(out=sg[:], in0=rec[:], scalar1=-0.5)
+            nc.vector.tensor_tensor(out=xf[:, 1, hi], in0=bst[:, 0:HALF], in1=bst[:, 0:HALF], op=ALU.mult)
+            nc.vector.tensor_tensor(out=xf[:, 1, lo], in0=bst[:, HALF:PLANES], in1=bst[:, HALF:PLANES], op=ALU.mult)
+            nc.vector.scalar_tensor_tensor(
+                out=xf[:, 1, r], in0=xf[:, 3, r], scalar=1.0 / (16.0 * pi2), in1=xf[:, 3, r], op0=ALU.mult, op1=ALU.mult
+            )
+            nc.vector.tensor_tensor(out=xf[:, 4, c], in0=xf[:, 2, c], in1=xf[:, 2, c], op=ALU.mult)
+            nc.vector.tensor_scalar_mul(out=xf[:, 4, r], in0=rec[:], scalar1=-2.0 * pi2)
+            nc.vector.tensor_tensor(out=xf[:, 0, r], in0=xf[:, 1, r], in1=sg[:], op=ALU.mult)
+            nc.vector.scalar_tensor_tensor(
+                out=xf[:, 5, c], in0=xf[:, 4, c], scalar=4.0 * pi2, in1=xf[:, 1, c], op0=ALU.mult, op1=ALU.mult
+            )
+            nc.vector.tensor_tensor(out=xf[:, 2, r], in0=xf[:, 3, r], in1=sg[:], op=ALU.mult)
+            nc.vector.tensor_tensor(out=xf[:, 3, c], in0=xf[:, 2, c], in1=xf[:, 1, c], op=ALU.mult)
+            rest = xf
             for e in range(3):
-                pc = const.tile(shape, BF16, name="%s_p%d" % (name, e))
+                pc = const.tile([P, TERMS, wide], BF16, name="xf_p%d" % e)
                 nc.vector.tensor_copy(out=pc[:], in_=rest[:])
-                pieces.append(pc)
                 if e < 2:
-                    nxt = const.tile(shape, F32, name="%s_r%d" % (name, e))
+                    nxt = const.tile([P, TERMS, wide], F32, name="xf_r%d" % e)
                     nc.vector.tensor_tensor(out=nxt[:], in0=rest[:], in1=pc[:], op=ALU.subtract)
                     rest = nxt
-            return pieces
-
-        def prepare_rows():
-            xf = const.tile([P, TERMS, TILES], F32)
-            sg = const.tile([P, TILES], F32)
-            nc.vector.memset(xf[:, 5, :], 1.0)
-            nc.vector.tensor_scalar_mul(out=sg[:], in0=rec[:], scalar1=-0.5)
-            nc.vector.tensor_scalar_mul(out=xf[:, 4, :], in0=rec[:], scalar1=-2.0 * pi2)
-            nc.vector.scalar_tensor_tensor(
-                out=xf[:, 3, :], in0=rec[:], scalar=4.0 * pi2, in1=th[:, :, 0], op0=ALU.mult, op1=ALU.mult
-            )
-            nc.vector.scalar_tensor_tensor(
-                out=xf[:, 1, :], in0=xf[:, 3, :], scalar=1.0 / (16.0 * pi2), in1=xf[:, 3, :], op0=ALU.mult, op1=ALU.mult
-            )
-            nc.vector.tensor_tensor(out=xf[:, 0, :], in0=xf[:, 1, :], in1=sg[:], op=ALU.mult)
-            nc.vector.tensor_tensor(out=xf[:, 2, :], in0=xf[:, 3, :], in1=sg[:], op=ALU.mult)
-            pcs = split3(xf, [P, TERMS, TILES], "xf")
-            for blk, (e, f) in enumerate(COMBOS):
-                nc.vector.tensor_copy(
-                    out=rowq[:, :, blk * SLOT : blk * SLOT + TERMS], in_=pcs[e][:].rearrange("p f i -> p i f")
-                )
-
-        def prepare_coefficients():
-            cf = const.tile([P, TERMS, PLANES], F32)
-            lo = slice(0, HALF)
-            hi = slice(HALF, PLANES)
-            nc.vector.tensor_copy(
-                out=bmt[:].rearrange("p (t c) -> p t c", c=PASSES), in_=bm[:].rearrange("p c t -> p t c")
-            )
-            nc.vector.memset(cf[:, 0, :], 1.0)
-            nc.vector.tensor_tensor(out=cf[:, 1, hi], in0=bst[:, lo], in1=bst[:, lo], op=ALU.mult)
-            nc.vector.tensor_tensor(out=cf[:, 1, lo], in0=bst[:, hi], in1=bst[:, hi], op=ALU.mult)
-            nc.vector.tensor_copy(out=cf[:, 2, :], in_=bmt[:])
-            nc.vector.tensor_tensor(out=cf[:, 4, :], in0=bmt[:], in1=bmt[:], op=ALU.mult)
-            nc.vector.tensor_tensor(out=cf[:, 3, :], in0=bmt[:], in1=cf[:, 1, :], op=ALU.mult)
-            nc.vector.scalar_tensor_tensor(
-                out=cf[:, 5, :], in0=cf[:, 4, :], scalar=4.0 * pi2, in1=cf[:, 1, :], op0=ALU.mult, op1=ALU.mult
-            )
-            pcs = split3(cf, [P, TERMS, PLANES], "cf")
-            for blk, (e, f) in enumerate(COMBOS):
-                nc.vector.tensor_copy(
-                    out=cofq[:, :, blk * SLOT : blk * SLOT + TERMS], in_=pcs[f][:].rearrange("p f k -> p k f")
-                )
+                for blk, (er, ec) in enumerate(COMBOS):
+                    s = slice(blk * SLOT, blk * SLOT + TERMS)
+                    if er == e:
+                        nc.vector.tensor_copy(out=rowq[:, :, s], in_=pc[:, :, r].rearrange("p f i -> p i f"))
+                    if ec == e:
+                        nc.vector.tensor_copy(out=cofq[:, :, s], in_=pc[:, :, c].rearrange("p f k -> p k f"))
 
         def turn(dst, d0, src, s0):
             tp = ps_z.tile([P, 4, P], BF16, tag="z")
@@ -305,16 +310,17 @@ def tile_longtermattention_kernel(tc, theta, basis_mu, basis_sigma, Bv, out):
             if kind == "XB":
                 spread(xb, b2, "act", "d")
             elif kind == "KB":
-                nc.vector.tensor_scalar_mul(out=bmf[:], in0=bmt[:], scalar1=kappa)
+                nc.vector.tensor_scalar_mul(
+                    out=bmf[:].rearrange("p (t c) -> p t c", c=PASSES), in0=bm[:].rearrange("p c t -> p t c"), scalar1=kappa
+                )
                 nc.vector.scalar_tensor_tensor(
                     out=mu[:], in0=rec[:], scalar=-0.5 * kappa, in1=th[:, :, 0], op0=ALU.mult, op1=ALU.mult
                 )
                 spread(kb, bmf, "dve", "z")
             elif kind == "PREP":
-                prepare_coefficients()
+                prepare()
                 turn(cofT, 0, cofq, 0)
                 turn(cofT, 4, cofq, 4)
-                prepare_rows()
             elif kind == "TURN":
                 turn(rowsT, 4 * st[1], rowq, 4 * st[1])
             elif kind == "LN":
@@ -324,7 +330,7 @@ def tile_longtermattention_kernel(tc, theta, basis_mu, basis_sigma, Bv, out):
                 ll[i] = lt
             elif kind == "S":
                 i = st[1]
-                sst = pair.tile([P, HALF * P], F32)
+                sst = pair.tile([P, HALF * P], F32, tag="sst", align_bytes=64)
                 nc.gpsimd.tensor_tensor(
                     out=sst[:], in0=ll[i][:, 0 : HALF * P], in1=ll[i][:, HALF * P : PLANES * P], op=ALU.add
                 )
@@ -352,15 +358,14 @@ def tile_longtermattention_kernel(tc, theta, basis_mu, basis_sigma, Bv, out):
             elif kind == "B":
                 i = st[1]
                 if i in CLASSIC:
-                    for s in range(2):
-                        nc.vector.scalar_tensor_tensor(
-                            out=bb[i][:],
-                            in0=kbf,
-                            scalar=mu[:, i : i + 1],
-                            in1=bb[i][:],
-                            op0=ALU.subtract,
-                            op1=ALU.mult,
-                        )
+                    nc.vector.scalar_tensor_tensor(
+                        out=bb[i][:],
+                        in0=kbf,
+                        scalar=mu[:, i : i + 1],
+                        in1=bb[i][:],
+                        op0=ALU.subtract,
+                        op1=ALU.mult,
+                    )
                 else:
                     bt = prod.tile([P, PLANES * P], F32, tag="bt", align_bytes=64)
                     bb[i] = bt
@@ -410,19 +415,18 @@ def tile_longtermattention_kernel(tc, theta, basis_mu, basis_sigma, Bv, out):
                     in_=rb[i][:].rearrange("p c n t -> p (c n t)"),
                 )
             elif kind == "BVG":
-                c = st[1]
-                gt = results.tile([P, D, PACK], BF16, tag="ost", align_bytes=64)
+                s = st[1]
                 nc.vector.tensor_copy(
-                    out=gt[:].rearrange("p (m i) t -> p m t i", i=4),
-                    in_=raws[c][:].rearrange("p t (m i) -> p m t i", i=4),
+                    out=grps[s][:].rearrange("p (m i) t -> p m t i", i=4),
+                    in_=raws[s][:].rearrange("p t (m i) -> p m t i", i=4),
                 )
-                grp[c] = gt
             elif kind == "BVQ":
-                c = st[1]
+                c, w = st[1] // 2, st[1] % 2
+                cols = slice(w * BANK, (w + 1) * BANK)
                 nc.vector.quantize_mx(
-                    out=bvc[:, c, :].bitcast(FP8X4),
-                    scales=bvs[:, c, :],
-                    in_=grp[c][:].rearrange("p w t -> p (w t)"),
+                    out=bvc[:, c, cols].bitcast(FP8X4),
+                    scales=bvs[:, c, cols],
+                    in_=grps[st[1]][:].rearrange("p w t -> p (w t)"),
                 )
             elif kind == "MX":
                 i, tag = st[1], st[2]

@@ -27,8 +27,8 @@ SLOT = 8
 
 FLOPS = 2 * ROWS * NB * D
 
-SIZES = (14, 10, 8)
-CLASSIC = (4, 8, 13, 17, 22, 26, 30)
+SIZES = (14, 12, 6)
+CLASSIC = (5, 9, 13, 17, 21, 25, 29)
 GADD = ()
 D_BUFS = 4
 Z_BUFS = 4
@@ -47,6 +47,7 @@ ZL = 1
 FL = 2
 QL = 3
 RUN = 2
+BACK = 1
 KB_EARLY = False
 EV_ACT = (0, 0, 0)
 
@@ -133,6 +134,8 @@ def plan():
                     for k in runs[s]:
                         if part == 0 or k in CLASSIC:
                             steps.append(("B", k, part))
+            if s == 0:
+                drain(99, "dve")
             if 0 <= s - ZL < len(runs):
                 for k in runs[s - ZL]:
                     steps.append(("ZT", k))
@@ -153,12 +156,15 @@ def plan():
                     turned[q] = 1
                     steps.append(("TURN", q))
             logs(hi, hi + SIZES[gi + 1])
-            while mxt[0] < len(mxq):
-                passes()
-                drain(1, "dve")
+            while mxt[0] < len(mxq) - BACK:
+                passes(1)
+                drain(1 if len(pending) - taken[0] < 6 else 2, "dve")
             for k in range(hi, hi + RUN):
                 d2(k)
             drain(99, "dve")
+            tags[0] = ("z",)
+            passes(BACK)
+            tags[0] = ("d", "z")
         lo = hi
     n = 0
     while taken[0] < len(pending) or mxt[0] < len(mxq):

@@ -22,14 +22,14 @@ BANK = 512
 PLANES = PASSES * PACK
 HALF = PLANES // 2
 TERMS = 6
-COMBOS = ((0, 0), (1, 0), (2, 0), (0, 1), (1, 1), (0, 2))
-SLOT = 8
+COMBOS = ((0, 0), (0, 1), (0, 2), (1, 0), (1, 1), (2, 0))
+ROW_SLOTS = ((0, 3), (3, 5), (5, 6))
+COF_SLOTS = (((0, 6, 3), (5, 6, 1)), ((1, 5, 3),), ((2, 3, 1),))
 
 FLOPS = 2 * ROWS * NB * D
 
 SIZES = (14, 12, 6)
 CLASSIC = (5, 9, 13, 17, 21, 25, 29)
-GADD = ()
 D_BUFS = 4
 Z_BUFS = 4
 ACC_BUFS = 8
@@ -178,7 +178,6 @@ def tile_longtermattention_kernel(tc, theta, basis_mu, basis_sigma, Bv, out):
     nc = tc.nc
     out_v = out.rearrange("(p i) d -> p i d", i=TILES)
     kappa = math.sqrt(2.0 * math.pi)
-    pi2 = math.pi * math.pi
     with ExitStack() as ctx:
         ctx.enter_context(tc.manual_schedule())
         const = ctx.enter_context(tc.tile_pool(name="const", bufs=1))
@@ -226,16 +225,23 @@ def tile_longtermattention_kernel(tc, theta, basis_mu, basis_sigma, Bv, out):
         rowq = const.tile([P, TILES, P], BF16)
         nc.vector.memset(rowq[:].bitcast(I32), 0)
 
-        bst = const.tile([P, PLANES], F32)
-        nc.vector.tensor_copy(out=bst[:].rearrange("p (t c) -> p t c", c=PASSES), in_=bs[:].rearrange("p c t -> p t c"))
+        xf = const.tile([P, TERMS, TILES + PLANES], F32)
+        nc.vector.memset(xf[:, 5, 0:TILES], 1.0)
+        nc.vector.memset(xf[:, 0, TILES : TILES + PLANES], 1.0)
         b2 = const.tile([P, PLANES], F32)
+        bsa = bs[:].rearrange("p c t -> p t c")
         nc.vector.scalar_tensor_tensor(
-            out=b2[:], in0=bst[:], scalar=2.0 * math.pi, in1=bst[:], op0=ALU.mult, op1=ALU.mult
+            out=b2[:].rearrange("p (t c) -> p t c", c=PASSES),
+            in0=bsa,
+            scalar=2.0 * math.pi,
+            in1=bsa,
+            op0=ALU.mult,
+            op1=ALU.mult,
         )
-        rec = const.tile([P, TILES], F32)
-        nc.vector.reciprocal(out=rec[:], in_=th[:, :, 1])
+        rec = xf[:, 4, 0:TILES]
+        nc.vector.reciprocal(out=rec, in_=th[:, :, 1])
         xa = const.tile([P, TILES], F32)
-        nc.vector.tensor_scalar_mul(out=xa[:], in0=rec[:], scalar1=-math.pi)
+        nc.vector.tensor_scalar_mul(out=xa[:], in0=rec, scalar1=-math.pi)
         mu = const.tile([P, TILES], F32)
         bmf = const.tile([P, PLANES], F32)
 
@@ -248,49 +254,51 @@ def tile_longtermattention_kernel(tc, theta, basis_mu, basis_sigma, Bv, out):
         ll, ww, bb, d2, zz, rb, cod, scl, acc, ost = {}, {}, {}, {}, {}, {}, {}, {}, {}, {}
 
         def prepare():
-            wide = TILES + PLANES
-            xf = const.tile([P, TERMS, wide], F32)
-            sg = const.tile([P, TILES], F32)
             r = slice(0, TILES)
-            c = slice(TILES, wide)
-            lo = slice(TILES, TILES + HALF)
-            hi = slice(TILES + HALF, wide)
-            nc.vector.memset(xf[:, 5, r], 1.0)
-            nc.vector.memset(xf[:, 0, c], 1.0)
+            c = slice(TILES, TILES + PLANES)
+            half = [
+                xf[:, 1, TILES + e * HALF : TILES + (e + 1) * HALF].rearrange("p (t c) -> p t c", c=PASSES) for e in range(2)
+            ]
+            bsv = [bs[:, :, 2 * e : 2 * e + 2].rearrange("p c t -> p t c") for e in range(2)]
+            nc.vector.tensor_tensor(out=xf[:, 3, r], in0=rec, in1=th[:, :, 0], op=ALU.mult)
+            nc.vector.tensor_scalar_mul(
+                out=xf[:, 2, c].rearrange("p (t c) -> p t c", c=PASSES),
+                in0=bm[:].rearrange("p c t -> p t c"),
+                scalar1=4.0,
+            )
+            for e in range(2):
+                nc.vector.scalar_tensor_tensor(
+                    out=half[e], in0=bsv[1 - e], scalar=-2.0, in1=bsv[1 - e], op0=ALU.mult, op1=ALU.mult
+                )
+            nc.vector.tensor_tensor(out=xf[:, 1, r], in0=xf[:, 3, r], in1=xf[:, 3, r], op=ALU.mult)
             nc.vector.scalar_tensor_tensor(
-                out=xf[:, 3, r], in0=rec[:], scalar=4.0 * pi2, in1=th[:, :, 0], op0=ALU.mult, op1=ALU.mult
+                out=xf[:, 4, c], in0=xf[:, 2, c], scalar=0.25, in1=xf[:, 2, c], op0=ALU.mult, op1=ALU.mult
             )
-            nc.vector.tensor_copy(
-                out=xf[:, 2, c].rearrange("p (t c) -> p t c", c=PASSES), in_=bm[:].rearrange("p c t -> p t c")
-            )
-            nc.vector.tensor_scalar_mul(out=sg[:], in0=rec[:], scalar1=-0.5)
-            nc.vector.tensor_tensor(out=xf[:, 1, hi], in0=bst[:, 0:HALF], in1=bst[:, 0:HALF], op=ALU.mult)
-            nc.vector.tensor_tensor(out=xf[:, 1, lo], in0=bst[:, HALF:PLANES], in1=bst[:, HALF:PLANES], op=ALU.mult)
-            nc.vector.scalar_tensor_tensor(
-                out=xf[:, 1, r], in0=xf[:, 3, r], scalar=1.0 / (16.0 * pi2), in1=xf[:, 3, r], op0=ALU.mult, op1=ALU.mult
-            )
-            nc.vector.tensor_tensor(out=xf[:, 4, c], in0=xf[:, 2, c], in1=xf[:, 2, c], op=ALU.mult)
-            nc.vector.tensor_scalar_mul(out=xf[:, 4, r], in0=rec[:], scalar1=-2.0 * pi2)
-            nc.vector.tensor_tensor(out=xf[:, 0, r], in0=xf[:, 1, r], in1=sg[:], op=ALU.mult)
-            nc.vector.scalar_tensor_tensor(
-                out=xf[:, 5, c], in0=xf[:, 4, c], scalar=4.0 * pi2, in1=xf[:, 1, c], op0=ALU.mult, op1=ALU.mult
-            )
-            nc.vector.tensor_tensor(out=xf[:, 2, r], in0=xf[:, 3, r], in1=sg[:], op=ALU.mult)
+            nc.vector.tensor_tensor(out=xf[:, 2, r], in0=xf[:, 3, r], in1=rec, op=ALU.mult)
             nc.vector.tensor_tensor(out=xf[:, 3, c], in0=xf[:, 2, c], in1=xf[:, 1, c], op=ALU.mult)
+            nc.vector.tensor_tensor(out=xf[:, 0, r], in0=xf[:, 1, r], in1=rec, op=ALU.mult)
+            nc.vector.tensor_tensor(out=xf[:, 5, c], in0=xf[:, 4, c], in1=xf[:, 1, c], op=ALU.mult)
             rest = xf
             for e in range(3):
-                pc = const.tile([P, TERMS, wide], BF16, name="xf_p%d" % e)
+                pc = const.tile([P, TERMS, TILES + PLANES], BF16, name="xf_p%d" % e)
                 nc.vector.tensor_copy(out=pc[:], in_=rest[:])
                 if e < 2:
-                    nxt = const.tile([P, TERMS, wide], F32, name="xf_r%d" % e)
+                    nxt = const.tile([P, TERMS, TILES + PLANES], F32, name="xf_r%d" % e)
                     nc.vector.tensor_tensor(out=nxt[:], in0=rest[:], in1=pc[:], op=ALU.subtract)
                     rest = nxt
-                for blk, (er, ec) in enumerate(COMBOS):
-                    s = slice(blk * SLOT, blk * SLOT + TERMS)
-                    if er == e:
-                        nc.vector.tensor_copy(out=rowq[:, :, s], in_=pc[:, :, r].rearrange("p f i -> p i f"))
-                    if ec == e:
-                        nc.vector.tensor_copy(out=cofq[:, :, s], in_=pc[:, :, c].rearrange("p f k -> p k f"))
+                for first, stop, step in COF_SLOTS[e]:
+                    n = len(range(first, stop, step))
+                    nc.vector.tensor_copy(
+                        out=cofq[:, :, 0 : len(COMBOS) * TERMS].rearrange("p k (s f) -> p k s f", f=TERMS)[
+                            :, :, first:stop:step, :
+                        ],
+                        in_=pc[:, :, c].rearrange("p f k -> p k f").unsqueeze(2).to_broadcast([P, PLANES, n, TERMS]),
+                    )
+                s0, s1 = ROW_SLOTS[e]
+                nc.vector.tensor_copy(
+                    out=rowq[:, :, s0 * TERMS : s1 * TERMS].rearrange("p i (s f) -> p i s f", f=TERMS),
+                    in_=pc[:, :, r].rearrange("p f i -> p i f").unsqueeze(2).to_broadcast([P, TILES, s1 - s0, TERMS]),
+                )
 
         def turn(dst, d0, src, s0):
             tp = ps_z.tile([P, 4, P], BF16, tag="z")
@@ -320,7 +328,7 @@ def tile_longtermattention_kernel(tc, theta, basis_mu, basis_sigma, Bv, out):
                     out=bmf[:].rearrange("p (t c) -> p t c", c=PASSES), in0=bm[:].rearrange("p c t -> p t c"), scalar1=kappa
                 )
                 nc.vector.scalar_tensor_tensor(
-                    out=mu[:], in0=rec[:], scalar=-0.5 * kappa, in1=th[:, :, 0], op0=ALU.mult, op1=ALU.mult
+                    out=mu[:], in0=rec, scalar=-0.5 * kappa, in1=th[:, :, 0], op0=ALU.mult, op1=ALU.mult
                 )
                 spread(kb, bmf, "dve", "z")
             elif kind == "PREP":
@@ -376,8 +384,13 @@ def tile_longtermattention_kernel(tc, theta, basis_mu, basis_sigma, Bv, out):
                     bt = prod.tile([P, PLANES * P], F32, tag="bt", align_bytes=64)
                     bb[i] = bt
                     for e in range(2):
-                        nc.vector.tensor_tensor(
-                            out=bt[:, e * BANK : (e + 1) * BANK], in0=d2[(i, e)][:], in1=ww[i][:], op=ALU.mult
+                        nc.vector.scalar_tensor_tensor(
+                            out=bt[:, e * BANK : (e + 1) * BANK],
+                            in0=d2[(i, e)][:],
+                            scalar=-0.5 * math.pi * math.pi,
+                            in1=ww[i][:],
+                            op0=ALU.mult,
+                            op1=ALU.mult,
                         )
             elif kind == "GZ":
                 i = st[1]
@@ -389,15 +402,12 @@ def tile_longtermattention_kernel(tc, theta, basis_mu, basis_sigma, Bv, out):
                     for t in range(PACK):
                         k = PASSES * t + c
                         ks = slice(k * P, (k + 1) * P)
-                        if i in GADD:
-                            nc.tensor.transpose(zt[:, t, :], bb[i][:, ks], ident[:])
-                        else:
-                            nc.tensor.matmul(
-                                out=zt[:, t, :], lhsT=ll[i][:, ks], rhs=ident[:], start=True, stop=False, is_transpose=True
-                            )
-                            nc.tensor.matmul(
-                                out=zt[:, t, :], lhsT=bb[i][:, ks], rhs=ident[:], start=False, stop=True, is_transpose=True
-                            )
+                        nc.tensor.matmul(
+                            out=zt[:, t, :], lhsT=ll[i][:, ks], rhs=ident[:], start=True, stop=False, is_transpose=True
+                        )
+                        nc.tensor.matmul(
+                            out=zt[:, t, :], lhsT=bb[i][:, ks], rhs=ident[:], start=False, stop=True, is_transpose=True
+                        )
                     zz[(i, c)] = zt
             elif kind == "F":
                 i = st[1]

@@ -25,11 +25,15 @@ TERMS = 6
 COMBOS = ((0, 0), (0, 1), (0, 2), (1, 0), (1, 1), (2, 0))
 ROW_SLOTS = ((0, 3), (3, 5), (5, 6))
 COF_SLOTS = (((0, 6, 3), (5, 6, 1)), ((1, 5, 3),), ((2, 3, 1),))
+BV_PIECES = 2
 
 FLOPS = 2 * ROWS * NB * D
 
 SIZES = (14, 12, 6)
 CLASSIC = (5, 9, 13, 17, 21, 25, 29)
+GADD = ()
+HOLD = 0
+QPOS = 1
 D_BUFS = 4
 Z_BUFS = 4
 ACC_BUFS = 8
@@ -49,6 +53,10 @@ QL = 3
 RUN = 2
 BACK = 1
 KB_EARLY = False
+KB_STEP = -1
+BV_HEAD = 4
+BV_STEP = 1
+TURN_HEAD = 4
 EV_ACT = (0, 0, 0)
 
 
@@ -93,6 +101,9 @@ def plan():
                 steps.append(("TURN", i // 4))
             steps.append(("D2", i))
 
+    def sorted_run(run):
+        return [k for k in run if k not in GADD] + [k for k in run if k in GADD]
+
     def logs(lo, hi):
         for i in range(lo, hi):
             steps.append(("LN", i))
@@ -105,16 +116,18 @@ def plan():
         d2(k)
     if KB_EARLY:
         steps.append(("KB",))
-    for s in range(4):
-        steps.append(("BVG", s))
-    for s in range(4):
-        steps.append(("BVQ", s))
-    logs(0, SIZES[0])
-    for q in range(1, TILES // 4):
-        if q * 4 < SIZES[0]:
+    def turn(q):
+        if q < TILES // 4 and q not in turned:
             turned[q] = 1
             steps.append(("TURN", q))
-    if not KB_EARLY:
+
+    bv = [("BVG", s) for s in range(BV_PIECES)] + [("BVQ", s) for s in range(BV_PIECES)]
+    for s in range(BV_HEAD):
+        steps.append(bv.pop(0))
+    logs(0, SIZES[0])
+    for q in range(1, TURN_HEAD):
+        turn(q)
+    if not KB_EARLY and KB_STEP < 0:
         steps.append(("KB",))
     lo = 0
     for gi, size in enumerate(SIZES):
@@ -129,32 +142,52 @@ def plan():
             if s + WA < len(runs):
                 for k in runs[s + WA]:
                     steps.append(("W", k))
+            if 0 <= s - QL < len(runs) and QPOS == 0:
+                for k in runs[s - QL]:
+                    steps.append(("Q", k))
+                    mxq.append(k)
             if s < len(runs):
                 for part in range(2):
                     for k in runs[s]:
                         if part == 0 or k in CLASSIC:
                             steps.append(("B", k, part))
+                        if k in GADD and part == (1 if k in CLASSIC else 0):
+                            steps.append(("GZ", k))
+                        if QPOS == 2 and part == 0 and k == runs[s][0] and 0 <= s - QL < len(runs):
+                            for j in runs[s - QL]:
+                                steps.append(("Q", j))
+                                mxq.append(j)
             if s == 0:
                 drain(99, "dve")
+            if gi == 0 and s == KB_STEP:
+                steps.append(("KB",))
             if 0 <= s - ZL < len(runs):
-                for k in runs[s - ZL]:
+                for k in sorted_run(runs[s - ZL]):
                     steps.append(("ZT", k))
             if s + 1 < len(runs):
                 for k in runs[s + 1]:
                     d2(k)
+            if s + 2 < len(runs):
+                turn(runs[s + 2][0] // 4)
+            if gi == 0:
+                for e in range(BV_STEP):
+                    if bv:
+                        steps.append(bv.pop(0))
             if 0 <= s - FL < len(runs):
-                for k in runs[s - FL]:
+                for k in sorted_run(runs[s - FL]):
                     steps.append(("F", k))
             if 0 <= s - QL < len(runs):
                 for k in runs[s - QL]:
-                    steps.append(("Q", k))
-                    mxq.append(k)
+                    if QPOS == 1 or (QPOS == 2 and s >= len(runs)):
+                        steps.append(("Q", k))
+                        mxq.append(k)
+        while bv:
+            steps.append(bv.pop(0))
         tags[0] = ("d", "z")
         if not last:
             for q in range(TILES // 4):
-                if q not in turned and q * 4 < hi + SIZES[gi + 1]:
-                    turned[q] = 1
-                    steps.append(("TURN", q))
+                if q * 4 < hi + SIZES[gi + 1]:
+                    turn(q)
             logs(hi, hi + SIZES[gi + 1])
             while mxt[0] < len(mxq) - BACK:
                 passes(1)
@@ -199,15 +232,17 @@ def tile_longtermattention_kernel(tc, theta, basis_mu, basis_sigma, Bv, out):
         nc.sync.dma_start(out=bm[:], in_=basis_mu.rearrange("(c p t) -> p c t", p=P, t=PACK))
         raws = []
         grps = []
-        for s in range(4):
-            gt = pair.tile([P, BANK, PACK], BF16, tag="sst", align_bytes=64)
+        per = BV_PIECES // 2
+        bw = D // per
+        for s in range(BV_PIECES):
+            gt = results.tile([P, bw, PACK], BF16, tag="ost", align_bytes=64)
             grps.append(gt)
-        for s in range(4):
-            c, w = s // 2, s % 2
-            raw = pair.tile([P, PACK, BANK], BF16, tag="sst", align_bytes=64)
+        for s in range(BV_PIECES):
+            c, w = s // per, s % per
+            raw = (results if per == 1 else rows).tile([P, PACK, bw], BF16, tag="ost" if per == 1 else "rb", align_bytes=64)
             nc.sync.dma_start(
                 out=raw[:],
-                in_=Bv[c * P * PACK : (c + 1) * P * PACK, w * BANK : (w + 1) * BANK].rearrange("(p t) w -> p t w", t=PACK),
+                in_=Bv[c * P * PACK : (c + 1) * P * PACK, w * bw : (w + 1) * bw].rearrange("(p t) w -> p t w", t=PACK),
             )
             raws.append(raw)
 
@@ -345,6 +380,8 @@ def tile_longtermattention_kernel(tc, theta, basis_mu, basis_sigma, Bv, out):
             elif kind == "S":
                 i = st[1]
                 sst = pair.tile([P, HALF * P], F32, tag="sst", align_bytes=64)
+                if i == HOLD:
+                    nc.vector.memset(sst[:, 0:1], 0.0)
                 nc.gpsimd.tensor_tensor(
                     out=sst[:], in0=ll[i][:, 0 : HALF * P], in1=ll[i][:, HALF * P : PLANES * P], op=ALU.add
                 )
@@ -402,16 +439,19 @@ def tile_longtermattention_kernel(tc, theta, basis_mu, basis_sigma, Bv, out):
                     for t in range(PACK):
                         k = PASSES * t + c
                         ks = slice(k * P, (k + 1) * P)
-                        nc.tensor.matmul(
-                            out=zt[:, t, :], lhsT=ll[i][:, ks], rhs=ident[:], start=True, stop=False, is_transpose=True
-                        )
-                        nc.tensor.matmul(
-                            out=zt[:, t, :], lhsT=bb[i][:, ks], rhs=ident[:], start=False, stop=True, is_transpose=True
-                        )
+                        if i in GADD:
+                            nc.tensor.transpose(zt[:, t, :], bb[i][:, ks], ident[:])
+                        else:
+                            nc.tensor.matmul(
+                                out=zt[:, t, :], lhsT=ll[i][:, ks], rhs=ident[:], start=True, stop=False, is_transpose=True
+                            )
+                            nc.tensor.matmul(
+                                out=zt[:, t, :], lhsT=bb[i][:, ks], rhs=ident[:], start=False, stop=True, is_transpose=True
+                            )
                     zz[(i, c)] = zt
             elif kind == "F":
                 i = st[1]
-                rbt = rows.tile([P, PASSES, P, PACK], BF16, align_bytes=64)
+                rbt = rows.tile([P, PASSES, P, PACK], BF16, tag="rb", align_bytes=64)
                 rb[i] = rbt
                 for c in range(PASSES):
                     nc.scalar.activation(
@@ -437,8 +477,8 @@ def tile_longtermattention_kernel(tc, theta, basis_mu, basis_sigma, Bv, out):
                     in_=raws[s][:].rearrange("p t (m i) -> p m t i", i=4),
                 )
             elif kind == "BVQ":
-                c, w = st[1] // 2, st[1] % 2
-                cols = slice(w * BANK, (w + 1) * BANK)
+                c, w = st[1] // per, st[1] % per
+                cols = slice(w * bw, (w + 1) * bw)
                 nc.vector.quantize_mx(
                     out=bvc[:, c, cols].bitcast(FP8X4),
                     scales=bvs[:, c, cols],

import math
from contextlib import ExitStack

import concourse.mybir as mybir
from concourse.masks import make_identity

F32 = mybir.dt.float32
BF16 = mybir.dt.bfloat16
U32 = mybir.dt.uint32
I32 = mybir.dt.int32
U8 = mybir.dt.uint8
FP8X4 = mybir.dt.float8_e4m3fn_x4
AF = mybir.ActivationFunctionType
ALU = mybir.AluOpType

P = 128
ROWS, NB, D = 4096, 1024, 1024
PACK = 4
PASSES = NB // (P * PACK)
TILES = ROWS // P
BANK = 512
PLANES = PASSES * PACK
HALF = PLANES // 2
TERMS = 6
COMBOS = ((0, 0), (0, 1), (0, 2), (1, 0), (1, 1), (2, 0))
ROW_SLOTS = ((0, 3), (3, 5), (5, 6))
COF_SLOTS = (((0, 6, 3), (5, 6, 1)), ((1, 5, 3),), ((2, 3, 1),))
BV_PIECES = 2

FLOPS = 2 * ROWS * NB * D

SIZES = (14, 12, 6)
CLASSIC = (5, 9, 13, 17, 21, 25, 29)
GADD = ()
HOLD = 0
QPOS = 1
D_BUFS = 4
Z_BUFS = 4
ACC_BUFS = 8
L_BUFS = 16
S_BUFS = 8
B_BUFS = 7
R_BUFS = 6
C_BUFS = 18
O_BUFS = 4
WA = 1
EXP_MX = (0, 0, 0)
EV_STEP = (0, 0, 0)
TAIL_SPLIT = True
ZL = 1
FL = 2
QL = 3
RUN = 2
BACK = 1
KB_EARLY = False
KB_STEP = -1
BV_HEAD = 4
BV_STEP = 1
TURN_HEAD = 4
EV_ACT = (0, 0, 0)


def plan():
    steps = []
    pending = []
    taken = [0]
    done = {}
    mxq = []
    mxt = [0]
    turned = {}

    def drain(n, eng):
        for s in range(n):
            if taken[0] >= len(pending):
                return
            i, dh = pending[taken[0]]
            taken[0] += 1
            steps.append(("EV", i, dh, eng))
            tiles = 1 if i >= TILES - 2 else 2
            first = i - i % tiles
            done[first] = done.get(first, 0) + 1
            if done[first] == 2 * tiles:
                steps.append(("ST", first, first + tiles))

    tags = [("d", "z")]

    def passes(limit=99):
        n = 0
        while mxt[0] < len(mxq) and len(pending) - taken[0] <= ACC_BUFS - 2 and n < limit:
            i = mxq[mxt[0]]
            steps.append(("MX", i, tags[0][mxt[0] % len(tags[0])]))
            mxt[0] += 1
            n += 1
            pending.append((i, 0))
            pending.append((i, 1))

    def d2(i):
        if i < TILES and i not in CLASSIC:
            if i // 4 not in turned:
                turned[i // 4] = 1
                steps.append(("TURN", i // 4))
            steps.append(("D2", i))

    def sorted_run(run):
        return [k for k in run if k not in GADD] + [k for k in run if k in GADD]

    def logs(lo, hi):
        for i in range(lo, hi):
            steps.append(("LN", i))
            if i not in CLASSIC:
                steps.append(("S", i))

    steps.append(("XB",))
    steps.append(("PREP",))
    for k in range(RUN):
        d2(k)
    if KB_EARLY:
        steps.append(("KB",))
    def turn(q):
        if q < TILES // 4 and q not in turned:
            turned[q] = 1
            steps.append(("TURN", q))

    bv = [("BVG", s) for s in range(BV_PIECES)] + [("BVQ", s) for s in range(BV_PIECES)]
    for s in range(BV_HEAD):
        steps.append(bv.pop(0))
    logs(0, SIZES[0])
    for q in range(1, TURN_HEAD):
        turn(q)
    if not KB_EARLY and KB_STEP < 0:
        steps.append(("KB",))
    lo = 0
    for gi, size in enumerate(SIZES):
        hi = lo + size
        last = gi + 1 == len(SIZES)
        runs = [tuple(range(a, min(a + RUN, hi))) for a in range(lo, hi, RUN)]
        for s in range(len(runs) + QL):
            if s == 0:
                for w in range(min(WA, len(runs))):
                    for k in runs[w]:
                        steps.append(("W", k))
            if s + WA < len(runs):
                for k in runs[s + WA]:
                    steps.append(("W", k))
            if 0 <= s - QL < len(runs) and QPOS == 0:
                for k in runs[s - QL]:
                    steps.append(("Q", k))
                    mxq.append(k)
            if s < len(runs):
                for part in range(2):
                    for k in runs[s]:
                        if part == 0 or k in CLASSIC:
                            steps.append(("B", k, part))
                        if k in GADD and part == (1 if k in CLASSIC else 0):
                            steps.append(("GZ", k))
                        if QPOS == 2 and part == 0 and k == runs[s][0] and 0 <= s - QL < len(runs):
                            for j in runs[s - QL]:
                                steps.append(("Q", j))
                                mxq.append(j)
            if s == 0:
                drain(99, "dve")
            if gi == 0 and s == KB_STEP:
                steps.append(("KB",))
            if 0 <= s - ZL < len(runs):
                for k in sorted_run(runs[s - ZL]):
                    steps.append(("ZT", k))
            if s + 1 < len(runs):
                for k in runs[s + 1]:
                    d2(k)
            if s + 2 < len(runs):
                turn(runs[s + 2][0] // 4)
            if gi == 0:
                for e in range(BV_STEP):
                    if bv:
                        steps.append(bv.pop(0))
            if 0 <= s - FL < len(runs):
                for k in sorted_run(runs[s - FL]):
                    steps.append(("F", k))
            if 0 <= s - QL < len(runs):
                for k in runs[s - QL]:
                    if QPOS == 1 or (QPOS == 2 and s >= len(runs)):
                        steps.append(("Q", k))
                        mxq.append(k)
        while bv:
            steps.append(bv.pop(0))
        tags[0] = ("d", "z")
        if not last:
            for q in range(TILES // 4):
                if q * 4 < hi + SIZES[gi + 1]:
                    turn(q)
            logs(hi, hi + SIZES[gi + 1])
            while mxt[0] < len(mxq) - BACK:
                passes(1)
                drain(1 if len(pending) - taken[0] < 6 else 2, "dve")
            for k in range(hi, hi + RUN):
                d2(k)
            drain(99, "dve")
            tags[0] = ("z",)
            passes(BACK)
            tags[0] = ("d", "z")
        lo = hi
    n = 0
    while taken[0] < len(pending) or mxt[0] < len(mxq):
        passes()
        drain(1, "act" if n % 2 else "dve")
        n += 1
    return steps


def tile_longtermattention_kernel(tc, theta, basis_mu, basis_sigma, Bv, out):
    nc = tc.nc
    out_v = out.rearrange("(p i) d -> p i d", i=TILES)
    kappa = math.sqrt(2.0 * math.pi)
    with ExitStack() as ctx:
        ctx.enter_context(tc.manual_schedule())
        const = ctx.enter_context(tc.tile_pool(name="const", bufs=1))
        logs = ctx.enter_context(tc.tile_pool(name="logs", bufs=L_BUFS))
        pair = ctx.enter_context(tc.tile_pool(name="pair", bufs=S_BUFS))
        prod = ctx.enter_context(tc.tile_pool(name="prod", bufs=B_BUFS))
        rows = ctx.enter_context(tc.tile_pool(name="rows", bufs=R_BUFS))
        packed = ctx.enter_context(tc.tile_pool(name="packed", bufs=C_BUFS))
        results = ctx.enter_context(tc.tile_pool(name="results", bufs=O_BUFS))
        ps_d = ctx.enter_context(tc.psum_pool(name="ps_d", bufs=D_BUFS))
        ps_z = ctx.enter_context(tc.psum_pool(name="ps_z", bufs=Z_BUFS))
        banks = {"z": ps_z, "d": ps_d}

        th = const.tile([P, TILES, 2], BF16)
        nc.sync.dma_start(out=th[:], in_=theta.rearrange("(p i) two -> p i two", i=TILES))
        bs = const.tile([P, PASSES, PACK], BF16)
        nc.sync.dma_start(out=bs[:], in_=basis_sigma.rearrange("(c p t) -> p c t", p=P, t=PACK))
        bm = const.tile([P, PASSES, PACK], BF16)
        nc.sync.dma_start(out=bm[:], in_=basis_mu.rearrange("(c p t) -> p c t", p=P, t=PACK))
        raws = []
        grps = []
        per = BV_PIECES // 2
        bw = D // per
        for s in range(BV_PIECES):
            gt = results.tile([P, bw, PACK], BF16, tag="ost", align_bytes=64)
            grps.append(gt)
        for s in range(BV_PIECES):
            c, w = s // per, s % per
            raw = (results if per == 1 else rows).tile([P, PACK, bw], BF16, tag="ost" if per == 1 else "rb", align_bytes=64)
            nc.sync.dma_start(
                out=raw[:],
                in_=Bv[c * P * PACK : (c + 1) * P * PACK, w * bw : (w + 1) * bw].rearrange("(p t) w -> p t w", t=PACK),
            )
            raws.append(raw)

        ident = const.tile([P, P], F32)
        make_identity(nc, ident[:])
        identb = const.tile([P, P], BF16)
        make_identity(nc, identb[:])

        warm = const.tile([P, 1], F32)
        nc.vector.memset(warm[:], 1.0)
        warm2 = const.tile([P, 1], F32)
        nc.scalar.activation(out=warm2[:], in_=warm[:], func=AF.Ln)
        cofq = const.tile([P, PLANES, P], BF16)
        nc.vector.memset(cofq[:].bitcast(I32), 0)
        rowq = const.tile([P, TILES, P], BF16)
        nc.vector.memset(rowq[:].bitcast(I32), 0)

        xf = const.tile([P, TERMS, TILES + PLANES], F32)
        nc.vector.memset(xf[:, 5, 0:TILES], 1.0)
        nc.vector.memset(xf[:, 0, TILES : TILES + PLANES], 1.0)
        b2 = const.tile([P, PLANES], F32)
        bsa = bs[:].rearrange("p c t -> p t c")
        nc.vector.scalar_tensor_tensor(
            out=b2[:].rearrange("p (t c) -> p t c", c=PASSES),
            in0=bsa,
            scalar=2.0 * math.pi,
            in1=bsa,
            op0=ALU.mult,
            op1=ALU.mult,
        )
        rec = xf[:, 4, 0:TILES]
        nc.vector.reciprocal(out=rec, in_=th[:, :, 1])
        xa = const.tile([P, TILES], F32)
        nc.vector.tensor_scalar_mul(out=xa[:], in0=rec, scalar1=-math.pi)
        mu = const.tile([P, TILES], F32)
        bmf = const.tile([P, PLANES], F32)

        bvc = const.tile([P, PASSES, D], U32, align_bytes=64)
        bvs = const.tile([P, PASSES, D], U8, align_bytes=64)
        xb = const.tile([P, PLANES, P], F32)
        kb = const.tile([P, PLANES, P], F32)
        rowsT = const.tile([P, TILES, P], BF16)
        cofT = const.tile([P, PLANES, P], BF16)
        ll, ww, bb, d2, zz, rb, cod, scl, acc, ost = {}, {}, {}, {}, {}, {}, {}, {}, {}, {}

        def prepare():
            r = slice(0, TILES)
            c = slice(TILES, TILES + PLANES)
            half = [
                xf[:, 1, TILES + e * HALF : TILES + (e + 1) * HALF].rearrange("p (t c) -> p t c", c=PASSES) for e in range(2)
            ]
            bsv = [bs[:, :, 2 * e : 2 * e + 2].rearrange("p c t -> p t c") for e in range(2)]
            nc.vector.tensor_tensor(out=xf[:, 3, r], in0=rec, in1=th[:, :, 0], op=ALU.mult)
            nc.vector.tensor_scalar_mul(
                out=xf[:, 2, c].rearrange("p (t c) -> p t c", c=PASSES),
                in0=bm[:].rearrange("p c t -> p t c"),
                scalar1=4.0,
            )
            for e in range(2):
                nc.vector.scalar_tensor_tensor(
                    out=half[e], in0=bsv[1 - e], scalar=-2.0, in1=bsv[1 - e], op0=ALU.mult, op1=ALU.mult
                )
            nc.vector.tensor_tensor(out=xf[:, 1, r], in0=xf[:, 3, r], in1=xf[:, 3, r], op=ALU.mult)
            nc.vector.scalar_tensor_tensor(
                out=xf[:, 4, c], in0=xf[:, 2, c], scalar=0.25, in1=xf[:, 2, c], op0=ALU.mult, op1=ALU.mult
            )
            nc.vector.tensor_tensor(out=xf[:, 2, r], in0=xf[:, 3, r], in1=rec, op=ALU.mult)
            nc.vector.tensor_tensor(out=xf[:, 3, c], in0=xf[:, 2, c], in1=xf[:, 1, c], op=ALU.mult)
            nc.vector.tensor_tensor(out=xf[:, 0, r], in0=xf[:, 1, r], in1=rec, op=ALU.mult)
            nc.vector.tensor_tensor(out=xf[:, 5, c], in0=xf[:, 4, c], in1=xf[:, 1, c], op=ALU.mult)
            rest = xf
            for e in range(3):
                pc = const.tile([P, TERMS, TILES + PLANES], BF16, name="xf_p%d" % e)
                nc.vector.tensor_copy(out=pc[:], in_=rest[:])
                if e < 2:
                    nxt = const.tile([P, TERMS, TILES + PLANES], F32, name="xf_r%d" % e)
                    nc.vector.tensor_tensor(out=nxt[:], in0=rest[:], in1=pc[:], op=ALU.subtract)
                    rest = nxt
                for first, stop, step in COF_SLOTS[e]:
                    n = len(range(first, stop, step))
                    nc.vector.tensor_copy(
                        out=cofq[:, :, 0 : len(COMBOS) * TERMS].rearrange("p k (s f) -> p k s f", f=TERMS)[
                            :, :, first:stop:step, :
                        ],
                        in_=pc[:, :, c].rearrange("p f k -> p k f").unsqueeze(2).to_broadcast([P, PLANES, n, TERMS]),
                    )
                s0, s1 = ROW_SLOTS[e]
                nc.vector.tensor_copy(
                    out=rowq[:, :, s0 * TERMS : s1 * TERMS].rearrange("p i (s f) -> p i s f", f=TERMS),
                    in_=pc[:, :, r].rearrange("p f i -> p i f").unsqueeze(2).to_broadcast([P, TILES, s1 - s0, TERMS]),
                )

        def turn(dst, d0, src, s0):
            tp = ps_z.tile([P, 4, P], BF16, tag="z")
            for j in range(4):
                nc.tensor.transpose(tp[:, j, :], src[:, s0 + j, :], identb[:])
            nc.vector.tensor_copy(out=dst[:, d0 : d0 + 4, :], in_=tp[:])

        def spread(dst, src, eng, tag):
            for g in range(2):
                bk = banks[tag].tile([P, 4, P], F32, tag=tag)
                for j in range(4):
                    k = 4 * g + j
                    nc.tensor.transpose(bk[:, j, :], src[:, k : k + 1].to_broadcast([P, P]), ident[:])
                if eng == "act":
                    nc.scalar.copy(out=dst[:, 4 * g : 4 * g + 4, :], in_=bk[:])
                else:
                    nc.vector.tensor_copy(out=dst[:, 4 * g : 4 * g + 4, :], in_=bk[:])

        xbf = xb[:].rearrange("p k m -> p (k m)")
        kbf = kb[:].rearrange("p k m -> p (k m)")
        for st in plan():
            kind = st[0]
            if kind == "XB":
                spread(xb, b2, "act", "d")
            elif kind == "KB":
                nc.vector.tensor_scalar_mul(
                    out=bmf[:].rearrange("p (t c) -> p t c", c=PASSES), in0=bm[:].rearrange("p c t -> p t c"), scalar1=kappa
                )
                nc.vector.scalar_tensor_tensor(
                    out=mu[:], in0=rec, scalar=-0.5 * kappa, in1=th[:, :, 0], op0=ALU.mult, op1=ALU.mult
                )
                spread(kb, bmf, "dve", "z")
            elif kind == "PREP":
                prepare()
                turn(cofT, 0, cofq, 0)
                turn(cofT, 4, cofq, 4)
            elif kind == "TURN":
                turn(rowsT, 4 * st[1], rowq, 4 * st[1])
            elif kind == "LN":
                i = st[1]
                lt = logs.tile([P, PLANES * P], F32, align_bytes=64)
                nc.scalar.activation(out=lt[:], in_=xbf, func=AF.Ln, bias=xa[:, i : i + 1])
                ll[i] = lt
            elif kind == "S":
                i = st[1]
                sst = pair.tile([P, HALF * P], F32, tag="sst", align_bytes=64)
                if i == HOLD:
                    nc.vector.memset(sst[:, 0:1], 0.0)
                nc.gpsimd.tensor_tensor(
                    out=sst[:], in0=ll[i][:, 0 : HALF * P], in1=ll[i][:, HALF * P : PLANES * P], op=ALU.add
                )
                ww[i] = sst
            elif kind == "W":
                i = st[1]
                if i in CLASSIC:
                    bt = prod.tile([P, PLANES * P], F32, tag="bt", align_bytes=64)
                    bb[i] = bt
                    nc.scalar.activation(out=bt[:], in_=ll[i][:], func=AF.Exp, scale=-1.0)
                else:
                    nc.scalar.activation(out=ww[i][:], in_=ww[i][:], func=AF.Exp, scale=-1.0)
            elif kind == "D2":
                i = st[1]
                for e in range(2):
                    dt = ps_d.tile([P, BANK], F32, tag="d")
                    nc.tensor.matmul(
                        out=dt[:],
                        lhsT=rowsT[:, i, :],
                        rhs=cofT[:, e * HALF : (e + 1) * HALF, :].rearrange("r k m -> r (k m)"),
                        start=True,
                        stop=True,
                    )
                    d2[(i, e)] = dt
            elif kind == "B":
                i = st[1]
                if i in CLASSIC:
                    nc.vector.scalar_tensor_tensor(
                        out=bb[i][:],
                        in0=kbf,
                        scalar=mu[:, i : i + 1],
                        in1=bb[i][:],
                        op0=ALU.subtract,
                        op1=ALU.mult,
                    )
                else:
                    bt = prod.tile([P, PLANES * P], F32, tag="bt", align_bytes=64)
                    bb[i] = bt
                    for e in range(2):
                        nc.vector.scalar_tensor_tensor(
                            out=bt[:, e * BANK : (e + 1) * BANK],
                            in0=d2[(i, e)][:],
                            scalar=-0.5 * math.pi * math.pi,
                            in1=ww[i][:],
                            op0=ALU.mult,
                            op1=ALU.mult,
                        )
            elif kind == "GZ":
                i = st[1]
                nc.gpsimd.tensor_tensor(out=bb[i][:], in0=bb[i][:], in1=ll[i][:], op=ALU.add)
            elif kind == "ZT":
                i = st[1]
                for c in range(PASSES):
                    zt = ps_z.tile([P, PACK, P], F32, tag="z")
                    for t in range(PACK):
                        k = PASSES * t + c
                        ks = slice(k * P, (k + 1) * P)
                        if i in GADD:
                            nc.tensor.transpose(zt[:, t, :], bb[i][:, ks], ident[:])
                        else:
                            nc.tensor.matmul(
                                out=zt[:, t, :], lhsT=ll[i][:, ks], rhs=ident[:], start=True, stop=False, is_transpose=True
                            )
                            nc.tensor.matmul(
                                out=zt[:, t, :], lhsT=bb[i][:, ks], rhs=ident[:], start=False, stop=True, is_transpose=True
                            )
                    zz[(i, c)] = zt
            elif kind == "F":
                i = st[1]
                rbt = rows.tile([P, PASSES, P, PACK], BF16, tag="rb", align_bytes=64)
                rb[i] = rbt
                for c in range(PASSES):
                    nc.scalar.activation(
                        out=rbt[:, c, :, :],
                        in_=zz[(i, c)][:].rearrange("p t n -> p n t"),
                        func=AF.Exp,
                        scale=-0.5,
                    )
            elif kind == "Q":
                i = st[1]
                cdt = packed.tile([P, PASSES * P], U32, align_bytes=64)
                sct = packed.tile([P, PASSES * P], U8, align_bytes=64)
                cod[i], scl[i] = cdt, sct
                nc.vector.quantize_mx(
                    out=cdt[:].bitcast(FP8X4),
                    scales=sct[:],
                    in_=rb[i][:].rearrange("p c n t -> p (c n t)"),
                )
            elif kind == "BVG":
                s = st[1]
                nc.vector.tensor_copy(
                    out=grps[s][:].rearrange("p (m i) t -> p m t i", i=4),
                    in_=raws[s][:].rearrange("p t (m i) -> p m t i", i=4),
                )
            elif kind == "BVQ":
                c, w = st[1] // per, st[1] % per
                cols = slice(w * bw, (w + 1) * bw)
                nc.vector.quantize_mx(
                    out=bvc[:, c, cols].bitcast(FP8X4),
                    scales=bvs[:, c, cols],
                    in_=grps[st[1]][:].rearrange("p w t -> p (w t)"),
                )
            elif kind == "MX":
                i, tag = st[1], st[2]
                for dh in range(D // BANK):
                    at = banks[tag].tile([P, BANK], F32, tag=tag)
                    dcols = slice(dh * BANK, (dh + 1) * BANK)
                    for c in range(PASSES):
                        cols = slice(c * P, (c + 1) * P)
                        nc.tensor.matmul_mx(
                            out=at[:],
                            lhsT=cod[i][:, cols].bitcast(FP8X4),
                            lhsT_scale=scl[i][:, cols],
                            rhs=bvc[:, c, dcols].bitcast(FP8X4),
                            rhs_scale=bvs[:, c, dcols],
                            start=(c == 0),
                            stop=(c == PASSES - 1),
                        )
                    acc[(i, dh)] = at
            elif kind == "EV":
                i, dh, eng = st[1], st[2], st[3]
                if i // 2 not in ost:
                    ot = results.tile([P, 2, D], F32, tag="ost", align_bytes=64)
                    ost[i // 2] = ot
                dst = ost[i // 2][:, i % 2, dh * BANK : (dh + 1) * BANK]
                if eng == "act":
                    nc.scalar.copy(out=dst, in_=acc[(i, dh)][:])
                else:
                    nc.vector.tensor_copy(out=dst, in_=acc[(i, dh)][:])
            elif kind == "ST":
                i0, i1 = st[1], st[2]
                nc.sync.dma_start(
                    out=out_v[:, i0:i1, :], in_=ost[i0 // 2][:, i0 % 2 : i0 % 2 + i1 - i0, :]
                )
